import numpy as np
import ml_dtypes


def mxq(x, axis, fmt="e4m3"):
    dtype, down = {"e4m3": (ml_dtypes.float8_e4m3fn, 7), "e5m2": (ml_dtypes.float8_e5m2, 14)}[fmt]
    v = np.moveaxis(np.asarray(x, np.float32).astype(ml_dtypes.bfloat16).astype(np.float64), axis, -1)
    blocks = v.reshape(v.shape[:-1] + (-1, 32))
    amax = np.abs(blocks).max(-1, keepdims=True)
    byte = np.maximum(np.where(amax > 0, np.frexp(amax)[1] - 1 + 127, 0) - down, 1)
    scale = np.exp2(byte - 127.0)
    codes = (blocks / scale).astype(np.float32).astype(dtype).astype(np.float64)
    return np.moveaxis((codes * scale).reshape(v.shape), -1, axis)


WIDE = False


def mx_kscale(k):
    if not WIDE:
        return np.ones(k)
    levels = np.array([10, -10, 5, -5, 0])
    a = np.random.permutation(np.resize(levels, k // 512 * 4)).reshape(k // 512, 4)
    idx = np.arange(k)
    return np.exp2(a[idx // 512, idx % 128 // 32])


BF16 = ml_dtypes.bfloat16


def bf(x):
    return np.asarray(x, np.float32).astype(BF16)


def f64(x):
    return np.asarray(x).astype(np.float64)


B, T, D, H, NUM_LAYERS = 2, 2048, 1024, 512, 3
EPS = 1e-8


def setup_inputs():
    s = mx_kscale(D)
    return {"inv": bf(np.random.standard_normal((B, T, D)) * 0.5 * s),
            "Wk": bf(np.random.standard_normal((D, D)) * 2.0 / np.sqrt(D) / s[None, :]),
            "bk": bf(2.5 / np.sqrt(D) + 0.7 * np.random.standard_normal(D))}


def reference(inv, Wk, bk):
    flat = f64(inv).reshape(-1, D)
    out = (mxq(flat, 1, "e4m3") @ mxq(f64(Wk), 1, "e4m3").T) + f64(bk)
    sqrtD = np.sqrt(D)
    S = out.sum(-1, keepdims=True)
    norms = np.sqrt((out * out).sum(-1, keepdims=True))
    c = out * S / (np.maximum(np.abs(out) * sqrtD, EPS) * np.maximum(norms, EPS))
    diff = np.abs(c[1:] - c[:-1]).sum(0)
    return np.broadcast_to(diff, (D, D)).copy()

@@ -1,0 +1,330 @@
+from contextlib import ExitStack
+
+import concourse.mybir as mybir
+from concourse.masks import make_identity
+
+F32 = mybir.dt.float32
+BF16 = mybir.dt.bfloat16
+U32 = mybir.dt.uint32
+U8 = mybir.dt.uint8
+FP8X4 = mybir.dt.float8_e4m3fn_x4
+ALU = mybir.AluOpType
+ACT = mybir.ActivationFunctionType
+AX = mybir.AxisListType
+
+P = 128
+D = 1024
+TOKENS = 4096
+TPP = TOKENS // P
+NT = TPP + 1
+HALF = 512
+FLOPS = 2 * TOKENS * D * D
+
+GROUPS = [[2 * k, 2 * k + 1] for k in range(TPP // 2)] + [[TPP]]
+NG = len(GROUPS)
+BATCHES = [(0, 9), (9, 17), (17, 25), (25, 29), (29, 32)]
+NB = len(BATCHES)
+NPIECE = 3
+YCOLS = NB * 8 * NPIECE
+SIGN_MAG = 2.0 ** -64
+
+
+def tile_dispatcher_pa_t_kernel(tc, inv, Wk, bk, out):
+    nc = tc.nc
+    flat = inv.flatten_outer_dims()
+    xv = flat.rearrange("(p t) k -> p t k", t=TPP)
+    wv = Wk.rearrange("(j p) k -> p j k", p=P)
+
+    with ExitStack() as ctx:
+        const = ctx.enter_context(tc.tile_pool(name="const", bufs=1))
+        wprep = ctx.enter_context(tc.tile_pool(name="wprep", bufs=1))
+        xpool = ctx.enter_context(tc.tile_pool(name="xpool", bufs=4))
+        gpool = ctx.enter_context(tc.tile_pool(name="gpool", bufs=3))
+        cpool = ctx.enter_context(tc.tile_pool(name="cpool", bufs=3))
+        opool = ctx.enter_context(tc.tile_pool(name="opool", bufs=6))
+        spool = ctx.enter_context(tc.tile_pool(name="spool", bufs=8))
+        pst = ctx.enter_context(tc.psum_pool(name="pst", bufs=2))
+        psm = ctx.enter_context(tc.psum_pool(name="psm", bufs=5))
+        psa = ctx.enter_context(tc.psum_pool(name="psa", bufs=1))
+
+        ident = const.tile([P, P], F32)
+        make_identity(nc, ident[:])
+        ones = const.tile([P, P], BF16)
+        nc.vector.memset(ones[:], SIGN_MAG)
+        nhalf = const.tile([P, NT], F32)
+        nc.vector.memset(nhalf[:], -0.5)
+        bias = const.tile([P, D], BF16)
+        nc.scalar.dma_start(out=bias[:], in_=bk.partition_broadcast(P))
+
+        ctx.enter_context(tc.manual_schedule())
+
+        wraw = wprep.tile([P, 8 * D], BF16)
+        xlast = const.tile([P, D], BF16)
+        xraw = {}
+
+        def load_w(c):
+            nc.sync.dma_start(
+                out=wraw[:, c * 4 * D : (c + 1) * 4 * D].rearrange("p (j k) -> p j k", j=4),
+                in_=wv[:, 4 * c : 4 * c + 4, :],
+            )
+
+        def load_x(c):
+            xr = xpool.tile([P, 4 * D], BF16, tag="xr")
+            nc.sync.dma_start(
+                out=xr[:].rearrange("p (t k) -> p t k", t=4), in_=xv[:, 4 * c : 4 * c + 4, :]
+            )
+            xraw[c] = xr
+
+        load_w(0)
+        load_x(0)
+        load_w(1)
+        for c in range(1, 4):
+            load_x(c)
+
+        def words(t):
+            if t == TPP:
+                return xlast[:].bitcast(F32)
+            return xraw[t // 4][:].bitcast(F32)[:, (t % 4) * HALF : (t % 4 + 1) * HALF]
+
+        wg = wprep.tile([P, 2 * D * 4], BF16, align_bytes=64)
+        wgf = wg[:].bitcast(F32).rearrange("p (g r u) -> p g r u", g=2, u=2)
+        wrf = wraw[:].bitcast(F32)
+        wc = const.tile([P, 2 * D], U32, align_bytes=64)
+        ws = const.tile([P, 2 * D], U8, align_bytes=64)
+
+        def prep_w(j):
+            tp = pst.tile([P, 4, P], F32, tag="tp")
+            for c in range(4):
+                nc.tensor.transpose(tp[:, c, :], wrf[:, j * HALF + c * P : j * HALF + (c + 1) * P], ident[:])
+            dst = wgf[:, :, j * P : (j + 1) * P, :]
+            src = tp[:].rearrange("p (g u) r -> p g r u", u=2)
+            if j % 2 == 0:
+                nc.scalar.copy(out=dst, in_=src)
+            else:
+                nc.vector.tensor_copy(out=dst, in_=src)
+
+        def quant_w(h):
+            for g in range(2):
+                lo = g * D + h * HALF
+                nc.vector.quantize_mx(
+                    out=wc[:, lo : lo + HALF].bitcast(FP8X4),
+                    scales=ws[:, lo : lo + HALF],
+                    in_=wg[:, lo * 4 : (lo + HALF) * 4],
+                )
+
+        sacc = const.tile([P, 2 * NT], F32)
+        nsq = const.tile([P, NT], F32)
+
+        def small_tiles(owner):
+            got = {}
+            for nm in ("stot", "qcl", "rn", "rr"):
+                got[nm] = const.tile([P, NT], F32, name=owner + nm)
+            for nm in ("ds", "mx", "mn", "ab", "ef", "r1", "r2"):
+                got[nm] = const.tile([P, 2, TPP], F32, name=owner + nm)
+            got["cf"] = const.tile([P, 2, TPP, NPIECE], BF16, name=owner + "cf")
+            return got
+
+        pool_set = small_tiles("g")
+        vector_set = small_tiles("v")
+        junk = const.tile([P, D], BF16)
+        yall = const.tile([P, TPP, D], BF16)
+        acc = psa.tile([P, HALF], F32)
+
+        tps = {}
+        grp = {}
+        cods = {}
+        mmt = {}
+        signs = {}
+
+        def stage_t(k):
+            got = []
+            for t in GROUPS[k]:
+                tp = pst.tile([P, 4, P], F32, tag="tp")
+                src = words(t)
+                for c in range(4):
+                    nc.tensor.transpose(tp[:, c, :], src[:, c * P : (c + 1) * P], ident[:])
+                got.append(tp)
+            tps[k] = got
+
+        def stage_ev(k):
+            n = len(GROUPS[k])
+            gt = gpool.tile([P, n * D], BF16, tag="grp", align_bytes=64)
+            gf = gt[:].bitcast(F32).rearrange("p (a g r u) -> p a g r u", a=n, g=2, u=2)
+            for a in range(n):
+                nc.scalar.copy(out=gf[:, a], in_=tps[k][a][:].rearrange("p (g u) r -> p g r u", u=2))
+            grp[k] = gt
+
+        def stage_q(k):
+            n = len(GROUPS[k])
+            cod = cpool.tile([P, n * 256], U32, tag="cod", align_bytes=64)
+            scl = cpool.tile([P, n * 256], U8, tag="scl", align_bytes=64)
+            nc.vector.quantize_mx(out=cod[:].bitcast(FP8X4), scales=scl[:], in_=grp[k][:])
+            cods[k] = (cod, scl)
+
+        def stage_m(k):
+            cod, scl = cods[k]
+            got = []
+            for a in range(len(GROUPS[k])):
+                for h in range(2):
+                    mm = psm.tile([P, HALF], F32, tag="mm")
+                    for g in range(2):
+                        off = (a * 2 + g) * P
+                        lo = g * D + h * HALF
+                        nc.tensor.matmul_mx(
+                            out=mm[:],
+                            lhsT=cod[:, off : off + P].bitcast(FP8X4),
+                            lhsT_scale=scl[:, off : off + P],
+                            rhs=wc[:, lo : lo + HALF].bitcast(FP8X4),
+                            rhs_scale=ws[:, lo : lo + HALF],
+                            start=(g == 0),
+                            stop=(g == 1),
+                        )
+                    got.append(mm)
+            mmt[k] = got
+
+        def stage_e(k):
+            for a, t in enumerate(GROUPS[k]):
+                o = opool.tile([P, D], F32, tag="o")
+                for h in range(2):
+                    nc.vector.scalar_tensor_tensor(
+                        out=o[:, h * HALF : (h + 1) * HALF],
+                        in0=mmt[k][2 * a + h][:],
+                        scalar=1.0,
+                        in1=bias[:, h * HALF : (h + 1) * HALF],
+                        op0=ALU.mult,
+                        op1=ALU.add,
+                        accum_out=sacc[:, h * NT + t : h * NT + t + 1],
+                    )
+                sg = spool.tile([P, D], BF16, tag="sg")
+                if t % 2 == 0:
+                    eng = nc.gpsimd if t < TPP else nc.vector
+                    eng.tensor_scalar(
+                        out=sg[:], in0=o[:], scalar1=SIGN_MAG, scalar2=-SIGN_MAG, op0=ALU.min, op1=ALU.max
+                    )
+                nc.scalar.activation(out=junk[:], in_=o[:], func=ACT.Square, accum_out=nsq[:, t : t + 1])
+                if t % 2 == 1:
+                    nc.scalar.activation(out=sg[:], in_=o[:], func=ACT.Sign)
+                signs[t] = sg
+
+        def stage_p(k):
+            for pair in (2 * k - 1, 2 * k):
+                if 0 <= pair < TPP:
+                    nc.vector.tensor_tensor(
+                        out=yall[:, pair, :], in0=signs[pair][:], in1=signs[pair + 1][:], op=ALU.mult
+                    )
+
+        def chain(b):
+            lo, hi = BATCHES[b]
+            eng = nc.vector if b == NB - 1 else nc.gpsimd
+            st = vector_set if b == NB - 1 else pool_set
+            stot, qcl, rn, rr = st["stot"], st["qcl"], st["rn"], st["rr"]
+            ds, mx, mn, ab, ef = st["ds"], st["mx"], st["mn"], st["ab"], st["ef"]
+            r1, r2, cf = st["r1"], st["r2"], st["cf"]
+            n0 = lo
+            n1 = hi + 1
+            eng.tensor_tensor(out=stot[:, n0:n1], in0=sacc[:, n0:n1], in1=sacc[:, NT + n0 : NT + n1], op=ALU.add)
+            eng.tensor_scalar(out=qcl[:, n0:n1], in0=nsq[:, n0:n1], scalar1=1e-16, scalar2=None, op0=ALU.max)
+            nc.gpsimd.tensor_tensor(out=rn[:, n0:n1], in0=qcl[:, n0:n1], in1=nhalf[:, n0:n1], op=ALU.pow)
+            eng.tensor_tensor(out=rr[:, n0:n1], in0=stot[:, n0:n1], in1=rn[:, n0:n1], op=ALU.mult)
+            eng.tensor_tensor(out=ds[:, 0, lo:hi], in0=rr[:, lo + 1 : hi + 1], in1=rr[:, lo:hi], op=ALU.subtract)
+            eng.tensor_tensor(out=ds[:, 1, lo:hi], in0=rr[:, lo + 1 : hi + 1], in1=rr[:, lo:hi], op=ALU.add)
+            eng.tensor_scalar(out=mx[:, :, lo:hi], in0=ds[:, :, lo:hi], scalar1=0.0, scalar2=None, op0=ALU.max)
+            eng.tensor_scalar(out=mn[:, :, lo:hi], in0=ds[:, :, lo:hi], scalar1=0.0, scalar2=None, op0=ALU.min)
+            eng.tensor_tensor(out=ab[:, :, lo:hi], in0=mx[:, :, lo:hi], in1=mn[:, :, lo:hi], op=ALU.subtract)
+            eng.tensor_tensor(out=ef[:, 0, lo:hi], in0=ab[:, 0, lo:hi], in1=ab[:, 1, lo:hi], op=ALU.subtract)
+            eng.tensor_tensor(out=ef[:, 1, lo:hi], in0=ab[:, 0, lo:hi], in1=ab[:, 1, lo:hi], op=ALU.add)
+            eng.tensor_copy(out=cf[:, :, lo:hi, 0], in_=ef[:, :, lo:hi])
+            eng.tensor_tensor(out=r1[:, :, lo:hi], in0=ef[:, :, lo:hi], in1=cf[:, :, lo:hi, 0], op=ALU.subtract)
+            eng.tensor_copy(out=cf[:, :, lo:hi, 1], in_=r1[:, :, lo:hi])
+            eng.tensor_tensor(out=r2[:, :, lo:hi], in0=r1[:, :, lo:hi], in1=cf[:, :, lo:hi, 1], op=ALU.subtract)
+            eng.tensor_copy(out=cf[:, :, lo:hi, 2], in_=r2[:, :, lo:hi])
+
+        def weigh(b, part):
+            lo, hi = BATCHES[b]
+            cf = vector_set["cf"] if b == NB - 1 else pool_set["cf"]
+            for j in range(4 * part, 4 * part + 4):
+                col = (b * 8 + j) * NPIECE
+                for pair in range(lo, hi):
+                    nc.tensor.matmul(
+                        out=acc[:, col : col + NPIECE],
+                        lhsT=yall[:, pair, j * P : (j + 1) * P],
+                        rhs=cf[:, 0, pair, :],
+                        start=(pair == lo),
+                        stop=(pair == hi - 1),
+                    )
+            if part == 1:
+                nc.tensor.matmul(
+                    out=acc[:, YCOLS + lo * NPIECE : YCOLS + hi * NPIECE],
+                    lhsT=ones[:],
+                    rhs=cf[:, 1, lo:hi, :].rearrange("p t c -> p (t c)"),
+                    start=True,
+                    stop=True,
+                )
+
+        for j in range(4):
+            prep_w(j)
+        quant_w(0)
+        stage_t(0)
+        stage_ev(0)
+        for j in range(4, 8):
+            prep_w(j)
+        quant_w(1)
+        stage_q(0)
+        stage_t(1)
+        stage_ev(1)
+        stage_m(0)
+        stage_q(1)
+        stage_t(2)
+
+        for k in range(NG + 5):
+            if k % 2 == 0 and k // 2 + 4 < 8:
+                load_x(k // 2 + 4)
+            if k == 8:
+                nc.sync.dma_start(out=xlast[0 : P - 1, :], in_=xv[1:P, 0, :])
+                nc.sync.dma_start(out=xlast[P - 1 : P, :], in_=flat[TOKENS - 1 : TOKENS, :])
+            if k + 2 < NG:
+                stage_ev(k + 2)
+            if k < NG:
+                stage_e(k)
+            if k + 1 < NG:
+                stage_m(k + 1)
+            if k + 3 < NG:
+                stage_t(k + 3)
+            if 1 <= k <= NG:
+                stage_p(k - 1)
+            if k + 2 < NG:
+                stage_q(k + 2)
+            for b, (lo, hi) in enumerate(BATCHES):
+                if k == hi // 2 + 1:
+                    chain(b)
+                if k == hi // 2 + 3:
+                    weigh(b, 0)
+                if k == hi // 2 + 4:
+                    weigh(b, 1)
+
+        accy = acc[:, 0:YCOLS].rearrange("p (b j c) -> p j b c", b=NB, j=8, c=NPIECE)
+        ysum = const.tile([P, 8], F32)
+        cs = const.tile([P, 1], F32)
+        rep = const.tile([P, 8, P], F32)
+        res = const.tile([P, D], F32)
+        nc.vector.tensor_reduce(out=ysum[:], in_=accy, axis=AX.XY, op=ALU.add)
+        nc.vector.tensor_reduce(out=cs[:], in_=acc[:, YCOLS : YCOLS + TPP * NPIECE], axis=AX.X, op=ALU.add)
+        nc.vector.tensor_scalar(
+            out=rep[:],
+            in0=ysum[:].unsqueeze(2).to_broadcast([P, 8, P]),
+            scalar1=cs[:, 0:1],
+            scalar2=1.0 / (64.0 * SIGN_MAG),
+            op0=ALU.add,
+            op1=ALU.mult,
+        )
+        bcs = []
+        for h in range(2):
+            bc = psm.tile([P, HALF], F32, tag="mm")
+            for jj in range(4):
+                nc.tensor.transpose(bc[:, jj * P : (jj + 1) * P], rep[:, 4 * h + jj, :], ident[:])
+            bcs.append(bc)
+        nc.vector.tensor_copy(out=res[:, 0:HALF], in_=bcs[0][:])
+        nc.scalar.copy(out=res[:, HALF:D], in_=bcs[1][:])
+        for eb in range(8):
+            eng = nc.sync if eb % 2 == 0 else nc.scalar
+            eng.dma_start(out=out[eb * P : (eb + 1) * P, :], in_=res[:])

@@ -26,7 +26,6 @@ BATCHES = [(0, 9), (9, 17), (17, 25), (25, 29), (29, 32)]
 NB = len(BATCHES)
 NPIECE = 3
 YCOLS = NB * 8 * NPIECE
-SIGN_MAG = 2.0 ** -64
 
 
 def tile_dispatcher_pa_t_kernel(tc, inv, Wk, bk, out):
@@ -50,7 +49,7 @@ def tile_dispatcher_pa_t_kernel(tc, inv, Wk, bk, out):
         ident = const.tile([P, P], F32)
         make_identity(nc, ident[:])
         ones = const.tile([P, P], BF16)
-        nc.vector.memset(ones[:], SIGN_MAG)
+        nc.vector.memset(ones[:], 1.0)
         nhalf = const.tile([P, NT], F32)
         nc.vector.memset(nhalf[:], -0.5)
         bias = const.tile([P, D], BF16)
@@ -64,22 +63,25 @@ def tile_dispatcher_pa_t_kernel(tc, inv, Wk, bk, out):
 
         def load_w(c):
             nc.sync.dma_start(
-                out=wraw[:, c * 4 * D : (c + 1) * 4 * D].rearrange("p (j k) -> p j k", j=4),
-                in_=wv[:, 4 * c : 4 * c + 4, :],
+                out=wraw[:, c * 2 * D : (c + 1) * 2 * D].rearrange("p (j k) -> p j k", j=2),
+                in_=wv[:, 2 * c : 2 * c + 2, :],
             )
 
-        def load_x(c):
+        def load_x(c, parts):
             xr = xpool.tile([P, 4 * D], BF16, tag="xr")
-            nc.sync.dma_start(
-                out=xr[:].rearrange("p (t k) -> p t k", t=4), in_=xv[:, 4 * c : 4 * c + 4, :]
-            )
+            n = 4 // parts
+            for i in range(parts):
+                nc.sync.dma_start(
+                    out=xr[:, i * n * D : (i + 1) * n * D].rearrange("p (t k) -> p t k", t=n),
+                    in_=xv[:, 4 * c + i * n : 4 * c + (i + 1) * n, :],
+                )
             xraw[c] = xr
 
-        load_w(0)
-        load_x(0)
-        load_w(1)
+        for c in range(4):
+            load_w(c)
+        load_x(0, 2)
         for c in range(1, 4):
-            load_x(c)
+            load_x(c, 1)
 
         def words(t):
             if t == TPP:
@@ -146,13 +148,18 @@ def tile_dispatcher_pa_t_kernel(tc, inv, Wk, bk, out):
                 got.append(tp)
             tps[k] = got
 
-        def stage_ev(k):
+        def stage_ev(k, a):
             n = len(GROUPS[k])
-            gt = gpool.tile([P, n * D], BF16, tag="grp", align_bytes=64)
-            gf = gt[:].bitcast(F32).rearrange("p (a g r u) -> p a g r u", a=n, g=2, u=2)
-            for a in range(n):
-                nc.scalar.copy(out=gf[:, a], in_=tps[k][a][:].rearrange("p (g u) r -> p g r u", u=2))
-            grp[k] = gt
+            if a == 0:
+                gt = gpool.tile([P, n * D], BF16, tag="grp", align_bytes=64)
+                grp[k] = gt
+            if a < n:
+                gf = grp[k][:].bitcast(F32).rearrange("p (a g r u) -> p a g r u", a=n, g=2, u=2)
+                view = tps[k][a][:].rearrange("p (g u) r -> p g r u", u=2)
+                if a == 0:
+                    nc.scalar.copy(out=gf[:, a], in_=view)
+                else:
+                    nc.vector.tensor_copy(out=gf[:, a], in_=view)
 
         def stage_q(k):
             n = len(GROUPS[k])
@@ -196,14 +203,8 @@ def tile_dispatcher_pa_t_kernel(tc, inv, Wk, bk, out):
                         accum_out=sacc[:, h * NT + t : h * NT + t + 1],
                     )
                 sg = spool.tile([P, D], BF16, tag="sg")
-                if t % 2 == 0:
-                    eng = nc.gpsimd if t < TPP else nc.vector
-                    eng.tensor_scalar(
-                        out=sg[:], in0=o[:], scalar1=SIGN_MAG, scalar2=-SIGN_MAG, op0=ALU.min, op1=ALU.max
-                    )
                 nc.scalar.activation(out=junk[:], in_=o[:], func=ACT.Square, accum_out=nsq[:, t : t + 1])
-                if t % 2 == 1:
-                    nc.scalar.activation(out=sg[:], in_=o[:], func=ACT.Sign)
+                nc.scalar.activation(out=sg[:], in_=o[:], func=ACT.Sign)
                 signs[t] = sg
 
         def stage_p(k):
@@ -265,27 +266,31 @@ def tile_dispatcher_pa_t_kernel(tc, inv, Wk, bk, out):
             prep_w(j)
         quant_w(0)
         stage_t(0)
-        stage_ev(0)
+        stage_ev(0, 0)
+        stage_ev(0, 1)
         for j in range(4, 8):
             prep_w(j)
         quant_w(1)
         stage_q(0)
         stage_t(1)
-        stage_ev(1)
+        stage_ev(1, 0)
+        stage_ev(1, 1)
         stage_m(0)
         stage_q(1)
         stage_t(2)
 
         for k in range(NG + 5):
             if k % 2 == 0 and k // 2 + 4 < 8:
-                load_x(k // 2 + 4)
+                load_x(k // 2 + 4, 1)
             if k == 8:
                 nc.sync.dma_start(out=xlast[0 : P - 1, :], in_=xv[1:P, 0, :])
                 nc.sync.dma_start(out=xlast[P - 1 : P, :], in_=flat[TOKENS - 1 : TOKENS, :])
             if k + 2 < NG:
-                stage_ev(k + 2)
+                stage_ev(k + 2, 0)
             if k < NG:
                 stage_e(k)
+            if k + 2 < NG:
+                stage_ev(k + 2, 1)
             if k + 1 < NG:
                 stage_m(k + 1)
             if k + 3 < NG:
@@ -313,7 +318,7 @@ def tile_dispatcher_pa_t_kernel(tc, inv, Wk, bk, out):
             out=rep[:],
             in0=ysum[:].unsqueeze(2).to_broadcast([P, 8, P]),
             scalar1=cs[:, 0:1],
-            scalar2=1.0 / (64.0 * SIGN_MAG),
+            scalar2=1.0 / 64.0,
             op0=ALU.add,
             op1=ALU.mult,
         )

@@ -26,6 +26,7 @@ BATCHES = [(0, 9), (9, 17), (17, 25), (25, 29), (29, 32)]
 NB = len(BATCHES)
 NPIECE = 3
 YCOLS = NB * 8 * NPIECE
+SIGN_MAG = 2.0 ** -64
 
 
 def tile_dispatcher_pa_t_kernel(tc, inv, Wk, bk, out):
@@ -49,7 +50,7 @@ def tile_dispatcher_pa_t_kernel(tc, inv, Wk, bk, out):
         ident = const.tile([P, P], F32)
         make_identity(nc, ident[:])
         ones = const.tile([P, P], BF16)
-        nc.vector.memset(ones[:], 1.0)
+        nc.vector.memset(ones[:], SIGN_MAG)
         nhalf = const.tile([P, NT], F32)
         nc.vector.memset(nhalf[:], -0.5)
         bias = const.tile([P, D], BF16)
@@ -122,7 +123,8 @@ def tile_dispatcher_pa_t_kernel(tc, inv, Wk, bk, out):
             for nm in ("stot", "qcl", "rn", "rr"):
                 got[nm] = const.tile([P, NT], F32, name=owner + nm)
             for nm in ("ds", "mx", "mn", "ab", "ef", "r1", "r2"):
-                got[nm] = const.tile([P, 2, TPP], F32, name=owner + nm)
+                if owner == "g" or nm not in ("mx", "mn"):
+                    got[nm] = const.tile([P, 2, TPP], F32, name=owner + nm)
             got["cf"] = const.tile([P, 2, TPP, NPIECE], BF16, name=owner + "cf")
             return got
 
@@ -156,10 +158,7 @@ def tile_dispatcher_pa_t_kernel(tc, inv, Wk, bk, out):
             if a < n:
                 gf = grp[k][:].bitcast(F32).rearrange("p (a g r u) -> p a g r u", a=n, g=2, u=2)
                 view = tps[k][a][:].rearrange("p (g u) r -> p g r u", u=2)
-                if a == 0:
-                    nc.scalar.copy(out=gf[:, a], in_=view)
-                else:
-                    nc.vector.tensor_copy(out=gf[:, a], in_=view)
+                nc.scalar.copy(out=gf[:, a], in_=view)
 
         def stage_q(k):
             n = len(GROUPS[k])
@@ -190,6 +189,7 @@ def tile_dispatcher_pa_t_kernel(tc, inv, Wk, bk, out):
             mmt[k] = got
 
         def stage_e(k):
+            outs = {}
             for a, t in enumerate(GROUPS[k]):
                 o = opool.tile([P, D], F32, tag="o")
                 for h in range(2):
@@ -202,9 +202,16 @@ def tile_dispatcher_pa_t_kernel(tc, inv, Wk, bk, out):
                         op1=ALU.add,
                         accum_out=sacc[:, h * NT + t : h * NT + t + 1],
                     )
-                sg = spool.tile([P, D], BF16, tag="sg")
                 nc.scalar.activation(out=junk[:], in_=o[:], func=ACT.Square, accum_out=nsq[:, t : t + 1])
-                nc.scalar.activation(out=sg[:], in_=o[:], func=ACT.Sign)
+                outs[t] = o
+            for t in GROUPS[k]:
+                sg = spool.tile([P, D], BF16, tag="sg")
+                if t % 2 == 0:
+                    nc.vector.tensor_scalar(
+                        out=sg[:], in0=outs[t][:], scalar1=SIGN_MAG, scalar2=-SIGN_MAG, op0=ALU.min, op1=ALU.max
+                    )
+                else:
+                    nc.scalar.activation(out=sg[:], in_=outs[t][:], func=ACT.Sign)
                 signs[t] = sg
 
         def stage_p(k):
@@ -219,19 +226,25 @@ def tile_dispatcher_pa_t_kernel(tc, inv, Wk, bk, out):
             eng = nc.vector if b == NB - 1 else nc.gpsimd
             st = vector_set if b == NB - 1 else pool_set
             stot, qcl, rn, rr = st["stot"], st["qcl"], st["rn"], st["rr"]
-            ds, mx, mn, ab, ef = st["ds"], st["mx"], st["mn"], st["ab"], st["ef"]
+            ds, ab, ef = st["ds"], st["ab"], st["ef"]
+            mx, mn = pool_set["mx"], pool_set["mn"]
             r1, r2, cf = st["r1"], st["r2"], st["cf"]
             n0 = lo
             n1 = hi + 1
             eng.tensor_tensor(out=stot[:, n0:n1], in0=sacc[:, n0:n1], in1=sacc[:, NT + n0 : NT + n1], op=ALU.add)
-            eng.tensor_scalar(out=qcl[:, n0:n1], in0=nsq[:, n0:n1], scalar1=1e-16, scalar2=None, op0=ALU.max)
+            nc.gpsimd.tensor_scalar(out=qcl[:, n0:n1], in0=nsq[:, n0:n1], scalar1=1e-16, scalar2=None, op0=ALU.max)
             nc.gpsimd.tensor_tensor(out=rn[:, n0:n1], in0=qcl[:, n0:n1], in1=nhalf[:, n0:n1], op=ALU.pow)
             eng.tensor_tensor(out=rr[:, n0:n1], in0=stot[:, n0:n1], in1=rn[:, n0:n1], op=ALU.mult)
             eng.tensor_tensor(out=ds[:, 0, lo:hi], in0=rr[:, lo + 1 : hi + 1], in1=rr[:, lo:hi], op=ALU.subtract)
             eng.tensor_tensor(out=ds[:, 1, lo:hi], in0=rr[:, lo + 1 : hi + 1], in1=rr[:, lo:hi], op=ALU.add)
-            eng.tensor_scalar(out=mx[:, :, lo:hi], in0=ds[:, :, lo:hi], scalar1=0.0, scalar2=None, op0=ALU.max)
-            eng.tensor_scalar(out=mn[:, :, lo:hi], in0=ds[:, :, lo:hi], scalar1=0.0, scalar2=None, op0=ALU.min)
-            eng.tensor_tensor(out=ab[:, :, lo:hi], in0=mx[:, :, lo:hi], in1=mn[:, :, lo:hi], op=ALU.subtract)
+            if b == NB - 1:
+                nc.vector.scalar_tensor_tensor(
+                    out=ab[:, :, lo:hi], in0=ds[:, :, lo:hi], scalar=-1.0, in1=ds[:, :, lo:hi], op0=ALU.mult, op1=ALU.max
+                )
+            else:
+                eng.tensor_scalar(out=mx[:, :, lo:hi], in0=ds[:, :, lo:hi], scalar1=0.0, scalar2=None, op0=ALU.max)
+                eng.tensor_scalar(out=mn[:, :, lo:hi], in0=ds[:, :, lo:hi], scalar1=0.0, scalar2=None, op0=ALU.min)
+                eng.tensor_tensor(out=ab[:, :, lo:hi], in0=mx[:, :, lo:hi], in1=mn[:, :, lo:hi], op=ALU.subtract)
             eng.tensor_tensor(out=ef[:, 0, lo:hi], in0=ab[:, 0, lo:hi], in1=ab[:, 1, lo:hi], op=ALU.subtract)
             eng.tensor_tensor(out=ef[:, 1, lo:hi], in0=ab[:, 0, lo:hi], in1=ab[:, 1, lo:hi], op=ALU.add)
             eng.tensor_copy(out=cf[:, :, lo:hi, 0], in_=ef[:, :, lo:hi])
@@ -265,12 +278,12 @@ def tile_dispatcher_pa_t_kernel(tc, inv, Wk, bk, out):
         for j in range(4):
             prep_w(j)
         quant_w(0)
-        stage_t(0)
-        stage_ev(0, 0)
-        stage_ev(0, 1)
         for j in range(4, 8):
             prep_w(j)
+        stage_t(0)
         quant_w(1)
+        stage_ev(0, 0)
+        stage_ev(0, 1)
         stage_q(0)
         stage_t(1)
         stage_ev(1, 0)
@@ -279,7 +292,7 @@ def tile_dispatcher_pa_t_kernel(tc, inv, Wk, bk, out):
         stage_q(1)
         stage_t(2)
 
-        for k in range(NG + 5):
+        for k in range(NG + 6):
             if k % 2 == 0 and k // 2 + 4 < 8:
                 load_x(k // 2 + 4, 1)
             if k == 8:
@@ -287,10 +300,9 @@ def tile_dispatcher_pa_t_kernel(tc, inv, Wk, bk, out):
                 nc.sync.dma_start(out=xlast[P - 1 : P, :], in_=flat[TOKENS - 1 : TOKENS, :])
             if k + 2 < NG:
                 stage_ev(k + 2, 0)
+                stage_ev(k + 2, 1)
             if k < NG:
                 stage_e(k)
-            if k + 2 < NG:
-                stage_ev(k + 2, 1)
             if k + 1 < NG:
                 stage_m(k + 1)
             if k + 3 < NG:
@@ -302,9 +314,9 @@ def tile_dispatcher_pa_t_kernel(tc, inv, Wk, bk, out):
             for b, (lo, hi) in enumerate(BATCHES):
                 if k == hi // 2 + 1:
                     chain(b)
-                if k == hi // 2 + 3:
-                    weigh(b, 0)
                 if k == hi // 2 + 4:
+                    weigh(b, 0)
+                if k == hi // 2 + 5:
                     weigh(b, 1)
 
         accy = acc[:, 0:YCOLS].rearrange("p (b j c) -> p j b c", b=NB, j=8, c=NPIECE)
@@ -318,7 +330,7 @@ def tile_dispatcher_pa_t_kernel(tc, inv, Wk, bk, out):
             out=rep[:],
             in0=ysum[:].unsqueeze(2).to_broadcast([P, 8, P]),
             scalar1=cs[:, 0:1],
-            scalar2=1.0 / 64.0,
+            scalar2=1.0 / (64.0 * SIGN_MAG),
             op0=ALU.add,
             op1=ALU.mult,
         )

@@ -20,11 +20,10 @@ NT = TPP + 1
 HALF = 512
 FLOPS = 2 * TOKENS * D * D
 
-GROUPS = [[2 * k, 2 * k + 1] for k in range(TPP // 2)] + [[TPP]]
-NG = len(GROUPS)
 BATCHES = [(0, 9), (9, 17), (17, 25), (25, 29), (29, 32)]
 NB = len(BATCHES)
 NPIECE = 3
+NPART = 4
 YCOLS = NB * 8 * NPIECE
 SIGN_MAG = 2.0 ** -64
 
@@ -39,8 +38,8 @@ def tile_dispatcher_pa_t_kernel(tc, inv, Wk, bk, out):
         const = ctx.enter_context(tc.tile_pool(name="const", bufs=1))
         wprep = ctx.enter_context(tc.tile_pool(name="wprep", bufs=1))
         xpool = ctx.enter_context(tc.tile_pool(name="xpool", bufs=4))
-        gpool = ctx.enter_context(tc.tile_pool(name="gpool", bufs=3))
-        cpool = ctx.enter_context(tc.tile_pool(name="cpool", bufs=3))
+        gpool = ctx.enter_context(tc.tile_pool(name="gpool", bufs=4))
+        cpool = ctx.enter_context(tc.tile_pool(name="cpool", bufs=4))
         opool = ctx.enter_context(tc.tile_pool(name="opool", bufs=6))
         spool = ctx.enter_context(tc.tile_pool(name="spool", bufs=8))
         pst = ctx.enter_context(tc.psum_pool(name="pst", bufs=2))
@@ -140,86 +139,70 @@ def tile_dispatcher_pa_t_kernel(tc, inv, Wk, bk, out):
         mmt = {}
         signs = {}
 
-        def stage_t(k):
+        def stage_t(t):
+            tp = pst.tile([P, 4, P], F32, tag="tp")
+            src = words(t)
+            for c in range(4):
+                nc.tensor.transpose(tp[:, c, :], src[:, c * P : (c + 1) * P], ident[:])
+            tps[t] = tp
+
+        def stage_ev(t):
+            gt = gpool.tile([P, D], BF16, tag="grp", align_bytes=64)
+            gf = gt[:].bitcast(F32).rearrange("p (g r u) -> p g r u", g=2, u=2)
+            nc.scalar.copy(out=gf, in_=tps[t][:].rearrange("p (g u) r -> p g r u", u=2))
+            grp[t] = gt
+
+        def stage_q(t):
+            cod = cpool.tile([P, 256], U32, tag="cod", align_bytes=64)
+            scl = cpool.tile([P, 256], U8, tag="scl", align_bytes=64)
+            nc.vector.quantize_mx(out=cod[:].bitcast(FP8X4), scales=scl[:], in_=grp[t][:])
+            cods[t] = (cod, scl)
+
+        def stage_m(t):
+            cod, scl = cods[t]
             got = []
-            for t in GROUPS[k]:
-                tp = pst.tile([P, 4, P], F32, tag="tp")
-                src = words(t)
-                for c in range(4):
-                    nc.tensor.transpose(tp[:, c, :], src[:, c * P : (c + 1) * P], ident[:])
-                got.append(tp)
-            tps[k] = got
-
-        def stage_ev(k, a):
-            n = len(GROUPS[k])
-            if a == 0:
-                gt = gpool.tile([P, n * D], BF16, tag="grp", align_bytes=64)
-                grp[k] = gt
-            if a < n:
-                gf = grp[k][:].bitcast(F32).rearrange("p (a g r u) -> p a g r u", a=n, g=2, u=2)
-                view = tps[k][a][:].rearrange("p (g u) r -> p g r u", u=2)
-                nc.scalar.copy(out=gf[:, a], in_=view)
-
-        def stage_q(k):
-            n = len(GROUPS[k])
-            cod = cpool.tile([P, n * 256], U32, tag="cod", align_bytes=64)
-            scl = cpool.tile([P, n * 256], U8, tag="scl", align_bytes=64)
-            nc.vector.quantize_mx(out=cod[:].bitcast(FP8X4), scales=scl[:], in_=grp[k][:])
-            cods[k] = (cod, scl)
-
-        def stage_m(k):
-            cod, scl = cods[k]
-            got = []
-            for a in range(len(GROUPS[k])):
-                for h in range(2):
-                    mm = psm.tile([P, HALF], F32, tag="mm")
-                    for g in range(2):
-                        off = (a * 2 + g) * P
-                        lo = g * D + h * HALF
-                        nc.tensor.matmul_mx(
-                            out=mm[:],
-                            lhsT=cod[:, off : off + P].bitcast(FP8X4),
-                            lhsT_scale=scl[:, off : off + P],
-                            rhs=wc[:, lo : lo + HALF].bitcast(FP8X4),
-                            rhs_scale=ws[:, lo : lo + HALF],
-                            start=(g == 0),
-                            stop=(g == 1),
-                        )
-                    got.append(mm)
-            mmt[k] = got
-
-        def stage_e(k):
-            outs = {}
-            for a, t in enumerate(GROUPS[k]):
-                o = opool.tile([P, D], F32, tag="o")
-                for h in range(2):
-                    nc.vector.scalar_tensor_tensor(
-                        out=o[:, h * HALF : (h + 1) * HALF],
-                        in0=mmt[k][2 * a + h][:],
-                        scalar=1.0,
-                        in1=bias[:, h * HALF : (h + 1) * HALF],
-                        op0=ALU.mult,
-                        op1=ALU.add,
-                        accum_out=sacc[:, h * NT + t : h * NT + t + 1],
+            for h in range(2):
+                mm = psm.tile([P, HALF], F32, tag="mm")
+                for g in range(2):
+                    lo = g * D + h * HALF
+                    nc.tensor.matmul_mx(
+                        out=mm[:],
+                        lhsT=cod[:, g * P : (g + 1) * P].bitcast(FP8X4),
+                        lhsT_scale=scl[:, g * P : (g + 1) * P],
+                        rhs=wc[:, lo : lo + HALF].bitcast(FP8X4),
+                        rhs_scale=ws[:, lo : lo + HALF],
+                        start=(g == 0),
+                        stop=(g == 1),
                     )
-                nc.scalar.activation(out=junk[:], in_=o[:], func=ACT.Square, accum_out=nsq[:, t : t + 1])
-                outs[t] = o
-            for t in GROUPS[k]:
-                sg = spool.tile([P, D], BF16, tag="sg")
-                if t % 2 == 0:
-                    nc.vector.tensor_scalar(
-                        out=sg[:], in0=outs[t][:], scalar1=SIGN_MAG, scalar2=-SIGN_MAG, op0=ALU.min, op1=ALU.max
-                    )
-                else:
-                    nc.scalar.activation(out=sg[:], in_=outs[t][:], func=ACT.Sign)
-                signs[t] = sg
+                got.append(mm)
+            mmt[t] = got
 
-        def stage_p(k):
-            for pair in (2 * k - 1, 2 * k):
-                if 0 <= pair < TPP:
-                    nc.vector.tensor_tensor(
-                        out=yall[:, pair, :], in0=signs[pair][:], in1=signs[pair + 1][:], op=ALU.mult
-                    )
+        def stage_e(t):
+            o = opool.tile([P, D], F32, tag="o")
+            for h in range(2):
+                nc.vector.scalar_tensor_tensor(
+                    out=o[:, h * HALF : (h + 1) * HALF],
+                    in0=mmt[t][h][:],
+                    scalar=1.0,
+                    in1=bias[:, h * HALF : (h + 1) * HALF],
+                    op0=ALU.mult,
+                    op1=ALU.add,
+                    accum_out=sacc[:, h * NT + t : h * NT + t + 1],
+                )
+            nc.scalar.activation(out=junk[:], in_=o[:], func=ACT.Square, accum_out=nsq[:, t : t + 1])
+            sg = spool.tile([P, D], BF16, tag="sg")
+            if t % 2 == 0:
+                nc.vector.tensor_scalar(
+                    out=sg[:], in0=o[:], scalar1=SIGN_MAG, scalar2=-SIGN_MAG, op0=ALU.min, op1=ALU.max
+                )
+            else:
+                nc.scalar.activation(out=sg[:], in_=o[:], func=ACT.Sign)
+            signs[t] = sg
+
+        def stage_p(pair):
+            nc.vector.tensor_tensor(
+                out=yall[:, pair, :], in0=signs[pair][:], in1=signs[pair + 1][:], op=ALU.mult
+            )
 
         def chain(b):
             lo, hi = BATCHES[b]
@@ -256,7 +239,8 @@ def tile_dispatcher_pa_t_kernel(tc, inv, Wk, bk, out):
         def weigh(b, part):
             lo, hi = BATCHES[b]
             cf = vector_set["cf"] if b == NB - 1 else pool_set["cf"]
-            for j in range(4 * part, 4 * part + 4):
+            nj = 8 // NPART
+            for j in range(nj * part, nj * (part + 1)):
                 col = (b * 8 + j) * NPIECE
                 for pair in range(lo, hi):
                     nc.tensor.matmul(
@@ -266,7 +250,7 @@ def tile_dispatcher_pa_t_kernel(tc, inv, Wk, bk, out):
                         start=(pair == lo),
                         stop=(pair == hi - 1),
                     )
-            if part == 1:
+            if part == NPART - 1:
                 nc.tensor.matmul(
                     out=acc[:, YCOLS + lo * NPIECE : YCOLS + hi * NPIECE],
                     lhsT=ones[:],
@@ -282,42 +266,43 @@ def tile_dispatcher_pa_t_kernel(tc, inv, Wk, bk, out):
             prep_w(j)
         stage_t(0)
         quant_w(1)
-        stage_ev(0, 0)
-        stage_ev(0, 1)
-        stage_q(0)
+        stage_ev(0)
         stage_t(1)
-        stage_ev(1, 0)
-        stage_ev(1, 1)
-        stage_m(0)
-        stage_q(1)
+        stage_ev(1)
+        stage_q(0)
         stage_t(2)
+        stage_ev(2)
+        stage_q(1)
+        stage_m(0)
+        stage_t(3)
 
-        for k in range(NG + 6):
-            if k % 2 == 0 and k // 2 + 4 < 8:
-                load_x(k // 2 + 4, 1)
-            if k == 8:
+        todo = [(b, part) for b in range(NB) for part in range(NPART)]
+        for k in range(NT + 2):
+            if k % 4 == 0 and k // 4 + 4 < 8:
+                load_x(k // 4 + 4, 1)
+            if k == 16:
                 nc.sync.dma_start(out=xlast[0 : P - 1, :], in_=xv[1:P, 0, :])
                 nc.sync.dma_start(out=xlast[P - 1 : P, :], in_=flat[TOKENS - 1 : TOKENS, :])
-            if k + 2 < NG:
-                stage_ev(k + 2, 0)
-                stage_ev(k + 2, 1)
-            if k < NG:
+            if k + 3 < NT:
+                stage_ev(k + 3)
+            if k < NT:
                 stage_e(k)
-            if k + 1 < NG:
+            if k + 1 < NT:
                 stage_m(k + 1)
-            if k + 3 < NG:
-                stage_t(k + 3)
-            if 1 <= k <= NG:
-                stage_p(k - 1)
-            if k + 2 < NG:
+            if k + 4 < NT:
+                stage_t(k + 4)
+            if 0 <= k - 2 < TPP:
+                stage_p(k - 2)
+            if k + 2 < NT:
                 stage_q(k + 2)
-            for b, (lo, hi) in enumerate(BATCHES):
-                if k == hi // 2 + 1:
+            for b in range(NB):
+                if k == BATCHES[b][1] + 1:
                     chain(b)
-                if k == hi // 2 + 4:
-                    weigh(b, 0)
-                if k == hi // 2 + 5:
-                    weigh(b, 1)
+            if todo and k >= BATCHES[todo[0][0]][1] + 5 + todo[0][1]:
+                weigh(todo[0][0], todo[0][1])
+                todo = todo[1:]
+        for b, part in todo:
+            weigh(b, part)
 
         accy = acc[:, 0:YCOLS].rearrange("p (b j c) -> p j b c", b=NB, j=8, c=NPIECE)
         ysum = const.tile([P, 8], F32)

@@ -20,10 +20,11 @@ NT = TPP + 1
 HALF = 512
 FLOPS = 2 * TOKENS * D * D
 
+GROUPS = [[2 * k, 2 * k + 1] for k in range(TPP // 2)] + [[TPP]]
+NG = len(GROUPS)
 BATCHES = [(0, 9), (9, 17), (17, 25), (25, 29), (29, 32)]
 NB = len(BATCHES)
 NPIECE = 3
-NPART = 4
 YCOLS = NB * 8 * NPIECE
 SIGN_MAG = 2.0 ** -64
 
@@ -38,8 +39,8 @@ def tile_dispatcher_pa_t_kernel(tc, inv, Wk, bk, out):
         const = ctx.enter_context(tc.tile_pool(name="const", bufs=1))
         wprep = ctx.enter_context(tc.tile_pool(name="wprep", bufs=1))
         xpool = ctx.enter_context(tc.tile_pool(name="xpool", bufs=4))
-        gpool = ctx.enter_context(tc.tile_pool(name="gpool", bufs=4))
-        cpool = ctx.enter_context(tc.tile_pool(name="cpool", bufs=4))
+        gpool = ctx.enter_context(tc.tile_pool(name="gpool", bufs=3))
+        cpool = ctx.enter_context(tc.tile_pool(name="cpool", bufs=3))
         opool = ctx.enter_context(tc.tile_pool(name="opool", bufs=6))
         spool = ctx.enter_context(tc.tile_pool(name="spool", bufs=8))
         pst = ctx.enter_context(tc.psum_pool(name="pst", bufs=2))
@@ -139,70 +140,83 @@ def tile_dispatcher_pa_t_kernel(tc, inv, Wk, bk, out):
         mmt = {}
         signs = {}
 
-        def stage_t(t):
-            tp = pst.tile([P, 4, P], F32, tag="tp")
-            src = words(t)
-            for c in range(4):
-                nc.tensor.transpose(tp[:, c, :], src[:, c * P : (c + 1) * P], ident[:])
-            tps[t] = tp
-
-        def stage_ev(t):
-            gt = gpool.tile([P, D], BF16, tag="grp", align_bytes=64)
-            gf = gt[:].bitcast(F32).rearrange("p (g r u) -> p g r u", g=2, u=2)
-            nc.scalar.copy(out=gf, in_=tps[t][:].rearrange("p (g u) r -> p g r u", u=2))
-            grp[t] = gt
-
-        def stage_q(t):
-            cod = cpool.tile([P, 256], U32, tag="cod", align_bytes=64)
-            scl = cpool.tile([P, 256], U8, tag="scl", align_bytes=64)
-            nc.vector.quantize_mx(out=cod[:].bitcast(FP8X4), scales=scl[:], in_=grp[t][:])
-            cods[t] = (cod, scl)
-
-        def stage_m(t):
-            cod, scl = cods[t]
+        def stage_t(k):
             got = []
-            for h in range(2):
-                mm = psm.tile([P, HALF], F32, tag="mm")
-                for g in range(2):
-                    lo = g * D + h * HALF
-                    nc.tensor.matmul_mx(
-                        out=mm[:],
-                        lhsT=cod[:, g * P : (g + 1) * P].bitcast(FP8X4),
-                        lhsT_scale=scl[:, g * P : (g + 1) * P],
-                        rhs=wc[:, lo : lo + HALF].bitcast(FP8X4),
-                        rhs_scale=ws[:, lo : lo + HALF],
-                        start=(g == 0),
-                        stop=(g == 1),
+            for t in GROUPS[k]:
+                tp = pst.tile([P, 4, P], F32, tag="tp")
+                src = words(t)
+                for c in range(4):
+                    nc.tensor.transpose(tp[:, c, :], src[:, c * P : (c + 1) * P], ident[:])
+                got.append(tp)
+            tps[k] = got
+
+        def stage_ev(k, a):
+            n = len(GROUPS[k])
+            if a == 0:
+                gt = gpool.tile([P, n * D], BF16, tag="grp", align_bytes=64)
+                grp[k] = gt
+            if a < n:
+                gf = grp[k][:].bitcast(F32).rearrange("p (a g r u) -> p a g r u", a=n, g=2, u=2)
+                view = tps[k][a][:].rearrange("p (g u) r -> p g r u", u=2)
+                nc.scalar.copy(out=gf[:, a], in_=view)
+
+        def stage_q(k):
+            n = len(GROUPS[k])
+            cod = cpool.tile([P, n * 256], U32, tag="cod", align_bytes=64)
+            scl = cpool.tile([P, n * 256], U8, tag="scl", align_bytes=64)
+            nc.vector.quantize_mx(out=cod[:].bitcast(FP8X4), scales=scl[:], in_=grp[k][:])
+            cods[k] = (cod, scl)
+
+        def stage_m(k):
+            cod, scl = cods[k]
+            got = []
+            for a in range(len(GROUPS[k])):
+                for h in range(2):
+                    mm = psm.tile([P, HALF], F32, tag="mm")
+                    for g in range(2):
+                        off = (a * 2 + g) * P
+                        lo = g * D + h * HALF
+                        nc.tensor.matmul_mx(
+                            out=mm[:],
+                            lhsT=cod[:, off : off + P].bitcast(FP8X4),
+                            lhsT_scale=scl[:, off : off + P],
+                            rhs=wc[:, lo : lo + HALF].bitcast(FP8X4),
+                            rhs_scale=ws[:, lo : lo + HALF],
+                            start=(g == 0),
+                            stop=(g == 1),
+                        )
+                    got.append(mm)
+            mmt[k] = got
+
+        def stage_e(k):
+            outs = {}
+            for a, t in enumerate(GROUPS[k]):
+                o = opool.tile([P, D], F32, tag="o")
+                for h in range(2):
+                    nc.vector.scalar_tensor_tensor(
+                        out=o[:, h * HALF : (h + 1) * HALF],
+                        in0=mmt[k][2 * a + h][:],
+                        scalar=1.0,
+                        in1=bias[:, h * HALF : (h + 1) * HALF],
+                        op0=ALU.mult,
+                        op1=ALU.add,
+                        accum_out=sacc[:, h * NT + t : h * NT + t + 1],
                     )
-                got.append(mm)
-            mmt[t] = got
+                nc.scalar.activation(out=junk[:], in_=o[:], func=ACT.Square, accum_out=nsq[:, t : t + 1])
+                outs[t] = o
+            for t in GROUPS[k]:
+                sg = spool.tile([P, D], BF16, tag="sg")
+                if t % 2 == 0:
+                    nc.vector.tensor_scalar(
+                        out=sg[:], in0=outs[t][:], scalar1=SIGN_MAG, scalar2=-SIGN_MAG, op0=ALU.min, op1=ALU.max
+                    )
+                else:
+                    nc.scalar.activation(out=sg[:], in_=outs[t][:], func=ACT.Sign)
+                signs[t] = sg
 
-        def stage_e(t):
-            o = opool.tile([P, D], F32, tag="o")
-            for h in range(2):
-                nc.vector.scalar_tensor_tensor(
-                    out=o[:, h * HALF : (h + 1) * HALF],
-                    in0=mmt[t][h][:],
-                    scalar=1.0,
-                    in1=bias[:, h * HALF : (h + 1) * HALF],
-                    op0=ALU.mult,
-                    op1=ALU.add,
-                    accum_out=sacc[:, h * NT + t : h * NT + t + 1],
-                )
-            nc.scalar.activation(out=junk[:], in_=o[:], func=ACT.Square, accum_out=nsq[:, t : t + 1])
-            sg = spool.tile([P, D], BF16, tag="sg")
-            if t % 2 == 0:
-                nc.vector.tensor_scalar(
-                    out=sg[:], in0=o[:], scalar1=SIGN_MAG, scalar2=-SIGN_MAG, op0=ALU.min, op1=ALU.max
-                )
-            else:
-                nc.scalar.activation(out=sg[:], in_=o[:], func=ACT.Sign)
-            signs[t] = sg
-
-        def stage_p(pair):
-            nc.vector.tensor_tensor(
-                out=yall[:, pair, :], in0=signs[pair][:], in1=signs[pair + 1][:], op=ALU.mult
-            )
+        def stage_p(eng, pair):
+            if 0 <= pair < TPP:
+                eng.tensor_tensor(out=yall[:, pair, :], in0=signs[pair][:], in1=signs[pair + 1][:], op=ALU.mult)
 
         def chain(b):
             lo, hi = BATCHES[b]
@@ -239,8 +253,7 @@ def tile_dispatcher_pa_t_kernel(tc, inv, Wk, bk, out):
         def weigh(b, part):
             lo, hi = BATCHES[b]
             cf = vector_set["cf"] if b == NB - 1 else pool_set["cf"]
-            nj = 8 // NPART
-            for j in range(nj * part, nj * (part + 1)):
+            for j in range(4 * part, 4 * part + 4):
                 col = (b * 8 + j) * NPIECE
                 for pair in range(lo, hi):
                     nc.tensor.matmul(
@@ -250,7 +263,7 @@ def tile_dispatcher_pa_t_kernel(tc, inv, Wk, bk, out):
                         start=(pair == lo),
                         stop=(pair == hi - 1),
                     )
-            if part == NPART - 1:
+            if part == 1:
                 nc.tensor.matmul(
                     out=acc[:, YCOLS + lo * NPIECE : YCOLS + hi * NPIECE],
                     lhsT=ones[:],
@@ -266,43 +279,43 @@ def tile_dispatcher_pa_t_kernel(tc, inv, Wk, bk, out):
             prep_w(j)
         stage_t(0)
         quant_w(1)
-        stage_ev(0)
-        stage_t(1)
-        stage_ev(1)
+        stage_ev(0, 0)
+        stage_ev(0, 1)
         stage_q(0)
-        stage_t(2)
-        stage_ev(2)
-        stage_q(1)
+        stage_t(1)
+        stage_ev(1, 0)
+        stage_ev(1, 1)
         stage_m(0)
-        stage_t(3)
+        stage_q(1)
+        stage_t(2)
 
-        todo = [(b, part) for b in range(NB) for part in range(NPART)]
-        for k in range(NT + 2):
-            if k % 4 == 0 and k // 4 + 4 < 8:
-                load_x(k // 4 + 4, 1)
-            if k == 16:
+        for k in range(NG + 6):
+            if k % 2 == 0 and k // 2 + 4 < 8:
+                load_x(k // 2 + 4, 1)
+            if k == 8:
                 nc.sync.dma_start(out=xlast[0 : P - 1, :], in_=xv[1:P, 0, :])
                 nc.sync.dma_start(out=xlast[P - 1 : P, :], in_=flat[TOKENS - 1 : TOKENS, :])
-            if k + 3 < NT:
-                stage_ev(k + 3)
-            if k < NT:
+            if k + 2 < NG:
+                stage_ev(k + 2, 0)
+                stage_ev(k + 2, 1)
+            if k < NG:
                 stage_e(k)
-            if k + 1 < NT:
+            if k + 1 < NG:
                 stage_m(k + 1)
-            if k + 4 < NT:
-                stage_t(k + 4)
-            if 0 <= k - 2 < TPP:
-                stage_p(k - 2)
-            if k + 2 < NT:
+            if k + 3 < NG:
+                stage_t(k + 3)
+            if k < NG:
+                stage_p(nc.vector, 2 * k - 1)
+                stage_p(nc.gpsimd, 2 * k)
+            if k + 2 < NG:
                 stage_q(k + 2)
-            for b in range(NB):
-                if k == BATCHES[b][1] + 1:
+            for b, (lo, hi) in enumerate(BATCHES):
+                if k == hi // 2 + 1:
                     chain(b)
-            if todo and k >= BATCHES[todo[0][0]][1] + 5 + todo[0][1]:
-                weigh(todo[0][0], todo[0][1])
-                todo = todo[1:]
-        for b, part in todo:
-            weigh(b, part)
+                if k == hi // 2 + 4:
+                    weigh(b, 0)
+                if k == hi // 2 + 5:
+                    weigh(b, 1)
 
         accy = acc[:, 0:YCOLS].rearrange("p (b j c) -> p j b c", b=NB, j=8, c=NPIECE)
         ysum = const.tile([P, 8], F32)

@@ -122,7 +122,7 @@ def tile_dispatcher_pa_t_kernel(tc, inv, Wk, bk, out):
             got = {}
             for nm in ("stot", "qcl", "rn", "rr"):
                 got[nm] = const.tile([P, NT], F32, name=owner + nm)
-            for nm in ("ds", "mx", "mn", "ab", "ef", "r1", "r2"):
+            for nm in ("ds", "mx", "mn", "ab", "ef", "r1"):
                 if owner == "g" or nm not in ("mx", "mn"):
                     got[nm] = const.tile([P, 2, TPP], F32, name=owner + nm)
             got["cf"] = const.tile([P, 2, TPP, NPIECE], BF16, name=owner + "cf")
@@ -214,9 +214,12 @@ def tile_dispatcher_pa_t_kernel(tc, inv, Wk, bk, out):
                     nc.scalar.activation(out=sg[:], in_=outs[t][:], func=ACT.Sign)
                 signs[t] = sg
 
-        def stage_p(eng, pair):
-            if 0 <= pair < TPP:
-                eng.tensor_tensor(out=yall[:, pair, :], in0=signs[pair][:], in1=signs[pair + 1][:], op=ALU.mult)
+        def stage_p(k):
+            for pair in (2 * k - 1, 2 * k):
+                if 0 <= pair < TPP:
+                    nc.vector.tensor_tensor(
+                        out=yall[:, pair, :], in0=signs[pair][:], in1=signs[pair + 1][:], op=ALU.mult
+                    )
 
         def chain(b):
             lo, hi = BATCHES[b]
@@ -225,7 +228,7 @@ def tile_dispatcher_pa_t_kernel(tc, inv, Wk, bk, out):
             stot, qcl, rn, rr = st["stot"], st["qcl"], st["rn"], st["rr"]
             ds, ab, ef = st["ds"], st["ab"], st["ef"]
             mx, mn = pool_set["mx"], pool_set["mn"]
-            r1, r2, cf = st["r1"], st["r2"], st["cf"]
+            r1, cf = st["r1"], st["cf"]
             n0 = lo
             n1 = hi + 1
             eng.tensor_tensor(out=stot[:, n0:n1], in0=sacc[:, n0:n1], in1=sacc[:, NT + n0 : NT + n1], op=ALU.add)
@@ -245,10 +248,9 @@ def tile_dispatcher_pa_t_kernel(tc, inv, Wk, bk, out):
             eng.tensor_tensor(out=ef[:, 0, lo:hi], in0=ab[:, 0, lo:hi], in1=ab[:, 1, lo:hi], op=ALU.subtract)
             eng.tensor_tensor(out=ef[:, 1, lo:hi], in0=ab[:, 0, lo:hi], in1=ab[:, 1, lo:hi], op=ALU.add)
             eng.tensor_copy(out=cf[:, :, lo:hi, 0], in_=ef[:, :, lo:hi])
+            eng.tensor_tensor(out=cf[:, :, lo:hi, 1], in0=ef[:, :, lo:hi], in1=cf[:, :, lo:hi, 0], op=ALU.subtract)
             eng.tensor_tensor(out=r1[:, :, lo:hi], in0=ef[:, :, lo:hi], in1=cf[:, :, lo:hi, 0], op=ALU.subtract)
-            eng.tensor_copy(out=cf[:, :, lo:hi, 1], in_=r1[:, :, lo:hi])
-            eng.tensor_tensor(out=r2[:, :, lo:hi], in0=r1[:, :, lo:hi], in1=cf[:, :, lo:hi, 1], op=ALU.subtract)
-            eng.tensor_copy(out=cf[:, :, lo:hi, 2], in_=r2[:, :, lo:hi])
+            eng.tensor_tensor(out=cf[:, :, lo:hi, 2], in0=r1[:, :, lo:hi], in1=cf[:, :, lo:hi, 1], op=ALU.subtract)
 
         def weigh(b, part):
             lo, hi = BATCHES[b]
@@ -304,9 +306,8 @@ def tile_dispatcher_pa_t_kernel(tc, inv, Wk, bk, out):
                 stage_m(k + 1)
             if k + 3 < NG:
                 stage_t(k + 3)
-            if k < NG:
-                stage_p(nc.vector, 2 * k - 1)
-                stage_p(nc.gpsimd, 2 * k)
+            if 1 <= k <= NG:
+                stage_p(k - 1)
             if k + 2 < NG:
                 stage_q(k + 2)
             for b, (lo, hi) in enumerate(BATCHES):
@@ -324,22 +325,26 @@ def tile_dispatcher_pa_t_kernel(tc, inv, Wk, bk, out):
         res = const.tile([P, D], F32)
         nc.vector.tensor_reduce(out=ysum[:], in_=accy, axis=AX.XY, op=ALU.add)
         nc.vector.tensor_reduce(out=cs[:], in_=acc[:, YCOLS : YCOLS + TPP * NPIECE], axis=AX.X, op=ALU.add)
-        nc.vector.tensor_scalar(
-            out=rep[:],
-            in0=ysum[:].unsqueeze(2).to_broadcast([P, 8, P]),
-            scalar1=cs[:, 0:1],
-            scalar2=1.0 / (64.0 * SIGN_MAG),
-            op0=ALU.add,
-            op1=ALU.mult,
-        )
         bcs = []
         for h in range(2):
+            nc.vector.tensor_scalar(
+                out=rep[:, 4 * h : 4 * h + 4, :],
+                in0=ysum[:, 4 * h : 4 * h + 4].unsqueeze(2).to_broadcast([P, 4, P]),
+                scalar1=cs[:, 0:1],
+                scalar2=1.0 / (64.0 * SIGN_MAG),
+                op0=ALU.add,
+                op1=ALU.mult,
+            )
             bc = psm.tile([P, HALF], F32, tag="mm")
             for jj in range(4):
                 nc.tensor.transpose(bc[:, jj * P : (jj + 1) * P], rep[:, 4 * h + jj, :], ident[:])
             bcs.append(bc)
         nc.vector.tensor_copy(out=res[:, 0:HALF], in_=bcs[0][:])
         nc.scalar.copy(out=res[:, HALF:D], in_=bcs[1][:])
-        for eb in range(8):
-            eng = nc.sync if eb % 2 == 0 else nc.scalar
-            eng.dma_start(out=out[eb * P : (eb + 1) * P, :], in_=res[:])
+        for h in range(2):
+            eng = nc.sync if h == 0 else nc.scalar
+            for eb in range(8):
+                eng.dma_start(
+                    out=out[eb * P : (eb + 1) * P, h * HALF : (h + 1) * HALF],
+                    in_=res[:, h * HALF : (h + 1) * HALF],
+                )

@@ -51,8 +51,9 @@ def tile_dispatcher_pa_t_kernel(tc, inv, Wk, bk, out):
         make_identity(nc, ident[:])
         ones = const.tile([P, P], BF16)
         nc.vector.memset(ones[:], SIGN_MAG)
-        nhalf = const.tile([P, NT], F32)
-        nc.vector.memset(nhalf[:], -0.5)
+        warm = const.tile([P, 2], F32)
+        nc.vector.memset(warm[:], 1.0)
+        nc.scalar.activation(out=warm[:, 1:2], in_=warm[:, 0:1], func=ACT.Sqrt)
         bias = const.tile([P, D], BF16)
         nc.scalar.dma_start(out=bias[:], in_=bk.partition_broadcast(P))
 
@@ -118,18 +119,17 @@ def tile_dispatcher_pa_t_kernel(tc, inv, Wk, bk, out):
         sacc = const.tile([P, 2 * NT], F32)
         nsq = const.tile([P, NT], F32)
 
-        def small_tiles(owner):
-            got = {}
-            for nm in ("stot", "qcl", "rn", "rr"):
-                got[nm] = const.tile([P, NT], F32, name=owner + nm)
-            for nm in ("ds", "mx", "mn", "ab", "ef", "r1"):
-                if owner == "g" or nm not in ("mx", "mn"):
-                    got[nm] = const.tile([P, 2, TPP], F32, name=owner + nm)
-            got["cf"] = const.tile([P, 2, TPP, NPIECE], BF16, name=owner + "cf")
-            return got
-
-        pool_set = small_tiles("g")
-        vector_set = small_tiles("v")
+        stot = const.tile([P, NT], F32)
+        nrm = const.tile([P, NT], F32)
+        ncl = const.tile([P, NT], F32)
+        rn = const.tile([P, NT], F32)
+        rr = const.tile([P, NT], F32)
+        ar = const.tile([P, NT], F32)
+        dd = const.tile([P, TPP], F32)
+        ad = const.tile([P, TPP], F32)
+        ef = const.tile([P, 2, TPP], F32)
+        r1 = const.tile([P, 2, TPP], F32)
+        cf = const.tile([P, 2, TPP, NPIECE], BF16)
         junk = const.tile([P, D], BF16)
         yall = const.tile([P, TPP, D], BF16)
         acc = psa.tile([P, HALF], F32)
@@ -202,6 +202,7 @@ def tile_dispatcher_pa_t_kernel(tc, inv, Wk, bk, out):
                         op1=ALU.add,
                         accum_out=sacc[:, h * NT + t : h * NT + t + 1],
                     )
+                trickle()
                 nc.scalar.activation(out=junk[:], in_=o[:], func=ACT.Square, accum_out=nsq[:, t : t + 1])
                 outs[t] = o
             for t in GROUPS[k]:
@@ -220,41 +221,44 @@ def tile_dispatcher_pa_t_kernel(tc, inv, Wk, bk, out):
                     nc.vector.tensor_tensor(
                         out=yall[:, pair, :], in0=signs[pair][:], in1=signs[pair + 1][:], op=ALU.mult
                     )
+                    trickle()
+
+        pending = []
 
         def chain(b):
             lo, hi = BATCHES[b]
-            eng = nc.vector if b == NB - 1 else nc.gpsimd
-            st = vector_set if b == NB - 1 else pool_set
-            stot, qcl, rn, rr = st["stot"], st["qcl"], st["rn"], st["rr"]
-            ds, ab, ef = st["ds"], st["ab"], st["ef"]
-            mx, mn = pool_set["mx"], pool_set["mn"]
-            r1, cf = st["r1"], st["cf"]
-            n0 = lo
-            n1 = hi + 1
-            eng.tensor_tensor(out=stot[:, n0:n1], in0=sacc[:, n0:n1], in1=sacc[:, NT + n0 : NT + n1], op=ALU.add)
-            nc.gpsimd.tensor_scalar(out=qcl[:, n0:n1], in0=nsq[:, n0:n1], scalar1=1e-16, scalar2=None, op0=ALU.max)
-            nc.gpsimd.tensor_tensor(out=rn[:, n0:n1], in0=qcl[:, n0:n1], in1=nhalf[:, n0:n1], op=ALU.pow)
-            eng.tensor_tensor(out=rr[:, n0:n1], in0=stot[:, n0:n1], in1=rn[:, n0:n1], op=ALU.mult)
-            eng.tensor_tensor(out=ds[:, 0, lo:hi], in0=rr[:, lo + 1 : hi + 1], in1=rr[:, lo:hi], op=ALU.subtract)
-            eng.tensor_tensor(out=ds[:, 1, lo:hi], in0=rr[:, lo + 1 : hi + 1], in1=rr[:, lo:hi], op=ALU.add)
-            if b == NB - 1:
-                nc.vector.scalar_tensor_tensor(
-                    out=ab[:, :, lo:hi], in0=ds[:, :, lo:hi], scalar=-1.0, in1=ds[:, :, lo:hi], op0=ALU.mult, op1=ALU.max
-                )
-            else:
-                eng.tensor_scalar(out=mx[:, :, lo:hi], in0=ds[:, :, lo:hi], scalar1=0.0, scalar2=None, op0=ALU.max)
-                eng.tensor_scalar(out=mn[:, :, lo:hi], in0=ds[:, :, lo:hi], scalar1=0.0, scalar2=None, op0=ALU.min)
-                eng.tensor_tensor(out=ab[:, :, lo:hi], in0=mx[:, :, lo:hi], in1=mn[:, :, lo:hi], op=ALU.subtract)
-            eng.tensor_tensor(out=ef[:, 0, lo:hi], in0=ab[:, 0, lo:hi], in1=ab[:, 1, lo:hi], op=ALU.subtract)
-            eng.tensor_tensor(out=ef[:, 1, lo:hi], in0=ab[:, 0, lo:hi], in1=ab[:, 1, lo:hi], op=ALU.add)
-            eng.tensor_copy(out=cf[:, :, lo:hi, 0], in_=ef[:, :, lo:hi])
-            eng.tensor_tensor(out=cf[:, :, lo:hi, 1], in0=ef[:, :, lo:hi], in1=cf[:, :, lo:hi, 0], op=ALU.subtract)
-            eng.tensor_tensor(out=r1[:, :, lo:hi], in0=ef[:, :, lo:hi], in1=cf[:, :, lo:hi, 0], op=ALU.subtract)
-            eng.tensor_tensor(out=cf[:, :, lo:hi, 2], in0=r1[:, :, lo:hi], in1=cf[:, :, lo:hi, 1], op=ALU.subtract)
+            new = slice(lo if b == 0 else lo + 1, hi + 1)
+            cur = slice(lo, hi)
+            nxt = slice(lo + 1, hi + 1)
+            v = nc.vector
+            return [
+                lambda: nc.scalar.activation(out=nrm[:, new], in_=nsq[:, new], func=ACT.Sqrt),
+                lambda: v.tensor_tensor(out=stot[:, new], in0=sacc[:, new], in1=sacc[:, NT + new.start : NT + new.stop], op=ALU.add),
+                lambda: v.tensor_scalar(out=ncl[:, new], in0=nrm[:, new], scalar1=1e-8, scalar2=None, op0=ALU.max),
+                lambda: v.reciprocal(out=rn[:, new], in_=ncl[:, new]),
+                lambda: v.tensor_tensor(out=rr[:, new], in0=stot[:, new], in1=rn[:, new], op=ALU.mult),
+                lambda: v.scalar_tensor_tensor(
+                    out=ar[:, new], in0=rr[:, new], scalar=-1.0, in1=rr[:, new], op0=ALU.mult, op1=ALU.max
+                ),
+                lambda: v.tensor_tensor(out=dd[:, cur], in0=rr[:, nxt], in1=rr[:, cur], op=ALU.subtract),
+                lambda: v.tensor_tensor(out=ef[:, 1, cur], in0=ar[:, nxt], in1=ar[:, cur], op=ALU.max),
+                lambda: v.scalar_tensor_tensor(
+                    out=ad[:, cur], in0=dd[:, cur], scalar=-1.0, in1=dd[:, cur], op0=ALU.mult, op1=ALU.max
+                ),
+                lambda: v.tensor_tensor(out=ef[:, 0, cur], in0=ad[:, cur], in1=ef[:, 1, cur], op=ALU.subtract),
+                lambda: v.tensor_copy(out=cf[:, :, cur, 0], in_=ef[:, :, cur]),
+                lambda: v.tensor_tensor(out=cf[:, :, cur, 1], in0=ef[:, :, cur], in1=cf[:, :, cur, 0], op=ALU.subtract),
+                lambda: v.tensor_tensor(out=r1[:, :, cur], in0=ef[:, :, cur], in1=cf[:, :, cur, 0], op=ALU.subtract),
+                lambda: v.tensor_tensor(out=cf[:, :, cur, 2], in0=r1[:, :, cur], in1=cf[:, :, cur, 1], op=ALU.subtract),
+            ]
+
+        def trickle(n=1):
+            for _ in range(n):
+                if pending:
+                    pending.pop(0)()
 
         def weigh(b, part):
             lo, hi = BATCHES[b]
-            cf = vector_set["cf"] if b == NB - 1 else pool_set["cf"]
             for j in range(4 * part, 4 * part + 4):
                 col = (b * 8 + j) * NPIECE
                 for pair in range(lo, hi):
@@ -291,7 +295,7 @@ def tile_dispatcher_pa_t_kernel(tc, inv, Wk, bk, out):
         stage_q(1)
         stage_t(2)
 
-        for k in range(NG + 6):
+        for k in range(NG + 7):
             if k % 2 == 0 and k // 2 + 4 < 8:
                 load_x(k // 2 + 4, 1)
             if k == 8:
@@ -312,10 +316,12 @@ def tile_dispatcher_pa_t_kernel(tc, inv, Wk, bk, out):
                 stage_q(k + 2)
             for b, (lo, hi) in enumerate(BATCHES):
                 if k == hi // 2 + 1:
-                    chain(b)
-                if k == hi // 2 + 4:
-                    weigh(b, 0)
+                    pending.extend(chain(b))
+                if k == NG:
+                    trickle(len(pending))
                 if k == hi // 2 + 5:
+                    weigh(b, 0)
+                if k == hi // 2 + 6:
                     weigh(b, 1)
 
         accy = acc[:, 0:YCOLS].rearrange("p (b j c) -> p j b c", b=NB, j=8, c=NPIECE)
@@ -331,7 +337,7 @@ def tile_dispatcher_pa_t_kernel(tc, inv, Wk, bk, out):
                 out=rep[:, 4 * h : 4 * h + 4, :],
                 in0=ysum[:, 4 * h : 4 * h + 4].unsqueeze(2).to_broadcast([P, 4, P]),
                 scalar1=cs[:, 0:1],
-                scalar2=1.0 / (64.0 * SIGN_MAG),
+                scalar2=1.0 / (32.0 * SIGN_MAG),
                 op0=ALU.add,
                 op1=ALU.mult,
             )

@@ -55,7 +55,11 @@ def tile_dispatcher_pa_t_kernel(tc, inv, Wk, bk, out):
         nc.vector.memset(warm[:], 1.0)
         nc.scalar.activation(out=warm[:, 1:2], in_=warm[:, 0:1], func=ACT.Sqrt)
         bias = const.tile([P, D], BF16)
-        nc.scalar.dma_start(out=bias[:], in_=bk.partition_broadcast(P))
+        unit = const.tile([P, P], BF16)
+        nc.gpsimd.memset(unit[:], 1.0)
+        brow = const.tile([P, D], BF16)
+        nc.vector.memset(brow[:], 0.0)
+        nc.scalar.dma_start(out=brow[0:1, :], in_=bk.rearrange("(o d) -> o d", o=1))
 
         ctx.enter_context(tc.manual_schedule())
 
@@ -278,6 +282,12 @@ def tile_dispatcher_pa_t_kernel(tc, inv, Wk, bk, out):
                     stop=True,
                 )
 
+        for h in range(2):
+            bb = psm.tile([P, HALF], F32, tag="mm")
+            nc.tensor.matmul(
+                out=bb[:], lhsT=unit[:], rhs=brow[:, h * HALF : (h + 1) * HALF], start=True, stop=True
+            )
+            nc.scalar.copy(out=bias[:, h * HALF : (h + 1) * HALF], in_=bb[:])
         for j in range(4):
             prep_w(j)
         quant_w(0)

@@ -16,17 +16,20 @@ P = 128
 D = 1024
 TOKENS = 4096
 TPP = TOKENS // P
-NT = TPP + 1
+NT = TPP
+NG = NT // 2
 HALF = 512
 FLOPS = 2 * TOKENS * D * D
 
-GROUPS = [[2 * k, 2 * k + 1] for k in range(TPP // 2)] + [[TPP]]
-NG = len(GROUPS)
-BATCHES = [(0, 9), (9, 17), (17, 25), (25, 29), (29, 32)]
+BATCHES = [(0, 8), (8, 16), (16, 24), (24, 28), (28, 32)]
 NB = len(BATCHES)
 NPIECE = 3
 YCOLS = NB * 8 * NPIECE
+RCOL = 256
 SIGN_MAG = 2.0 ** -64
+WARMUP = 4
+COOL = 8
+PARTS = [(0, 0), (0, 1), (1, 0), (1, 1)]
 
 
 def tile_dispatcher_pa_t_kernel(tc, inv, Wk, bk, out):
@@ -41,30 +44,49 @@ def tile_dispatcher_pa_t_kernel(tc, inv, Wk, bk, out):
         xpool = ctx.enter_context(tc.tile_pool(name="xpool", bufs=4))
         gpool = ctx.enter_context(tc.tile_pool(name="gpool", bufs=3))
         cpool = ctx.enter_context(tc.tile_pool(name="cpool", bufs=3))
-        opool = ctx.enter_context(tc.tile_pool(name="opool", bufs=6))
-        spool = ctx.enter_context(tc.tile_pool(name="spool", bufs=8))
+        opool = ctx.enter_context(tc.tile_pool(name="opool", bufs=5))
         pst = ctx.enter_context(tc.psum_pool(name="pst", bufs=2))
         psm = ctx.enter_context(tc.psum_pool(name="psm", bufs=5))
         psa = ctx.enter_context(tc.psum_pool(name="psa", bufs=1))
 
+        bcol = const.tile([P, 8], BF16)
+        nc.scalar.dma_start(out=bcol[:], in_=bk.rearrange("(p c) -> p c", c=8))
+        unit = const.tile([P, HALF], BF16)
+        nc.vector.memset(unit[:], 1.0)
         ident = const.tile([P, P], F32)
         make_identity(nc, ident[:])
         ones = const.tile([P, P], BF16)
-        nc.vector.memset(ones[:], SIGN_MAG)
+        nc.vector.memset(ones[:], 1.0)
         warm = const.tile([P, 2], F32)
         nc.vector.memset(warm[:], 1.0)
         nc.scalar.activation(out=warm[:, 1:2], in_=warm[:, 0:1], func=ACT.Sqrt)
         bias = const.tile([P, D], BF16)
-        unit = const.tile([P, P], BF16)
-        nc.gpsimd.memset(unit[:], 1.0)
-        brow = const.tile([P, D], BF16)
-        nc.vector.memset(brow[:], 0.0)
-        nc.scalar.dma_start(out=brow[0:1, :], in_=bk.rearrange("(o d) -> o d", o=1))
+        identb = const.tile([P, P], BF16)
+        nc.vector.tensor_copy(out=identb[:], in_=ident[:])
+        shift = const.tile([P, P], F32)
+        nc.vector.memset(shift[:], 0.0)
+        nc.vector.tensor_copy(out=shift[:, 0 : P - 1], in_=ident[:, 1:P])
+        shiftb = const.tile([P, P], BF16)
+        nc.vector.tensor_copy(out=shiftb[:], in_=shift[:])
+        most = const.tile([P, P], BF16)
+        nc.vector.tensor_scalar(
+            out=most[:],
+            in0=ident[:, P - 1 : P].to_broadcast([P, P]),
+            scalar1=-1.0,
+            scalar2=1.0,
+            op0=ALU.mult,
+            op1=ALU.add,
+        )
 
         ctx.enter_context(tc.manual_schedule())
 
-        wraw = wprep.tile([P, 8 * D], BF16)
-        xlast = const.tile([P, D], BF16)
+        wraw = wprep.tile([P, 8 * D], BF16, offset=0)
+        wleft = wprep.tile([P, 4 * D], BF16, align_bytes=64, offset=16 * D)
+        wright = wprep.tile([P, 4 * D], BF16, align_bytes=64, offset=24 * D)
+        wg = [wleft, wright]
+        wrf = wraw[:].bitcast(F32)
+        wc = const.tile([P, 2 * D], U32, align_bytes=64)
+        ws = const.tile([P, 2 * D], U8, align_bytes=64)
         xraw = {}
 
         def load_w(c):
@@ -73,40 +95,56 @@ def tile_dispatcher_pa_t_kernel(tc, inv, Wk, bk, out):
                 in_=wv[:, 2 * c : 2 * c + 2, :],
             )
 
-        def load_x(c, parts):
-            xr = xpool.tile([P, 4 * D], BF16, tag="xr")
-            n = 4 // parts
-            for i in range(parts):
-                nc.sync.dma_start(
-                    out=xr[:, i * n * D : (i + 1) * n * D].rearrange("p (t k) -> p t k", t=n),
-                    in_=xv[:, 4 * c + i * n : 4 * c + (i + 1) * n, :],
-                )
-            xraw[c] = xr
+        def load_x(c, u, v):
+            if u == 0:
+                xr = xpool.tile([P, 4 * D], BF16, tag="xr")
+                xraw[c] = xr
+            nc.sync.dma_start(
+                out=xraw[c][:, u * D : v * D].rearrange("p (t k) -> p t k", t=v - u),
+                in_=xv[:, 4 * c + u : 4 * c + v, :],
+            )
 
+        load_x(0, 0, 2)
         for c in range(4):
             load_w(c)
-        load_x(0, 2)
+        load_x(0, 2, 4)
         for c in range(1, 4):
-            load_x(c, 1)
+            load_x(c, 0, 4)
 
         def words(t):
-            if t == TPP:
-                return xlast[:].bitcast(F32)
             return xraw[t // 4][:].bitcast(F32)[:, (t % 4) * HALF : (t % 4 + 1) * HALF]
 
-        wg = wprep.tile([P, 2 * D * 4], BF16, align_bytes=64)
-        wgf = wg[:].bitcast(F32).rearrange("p (g r u) -> p g r u", g=2, u=2)
-        wrf = wraw[:].bitcast(F32)
-        wc = const.tile([P, 2 * D], U32, align_bytes=64)
-        ws = const.tile([P, 2 * D], U8, align_bytes=64)
+        sacc = const.tile([P, 2 * NT], F32)
+        nsq = const.tile([P, NT], F32)
+        stot = const.tile([P, NT], F32)
+        nrm = const.tile([P, NT], F32)
+        rn = const.tile([P, NT], F32)
+        rr = const.tile([P, NT + 1], F32)
+        ar = const.tile([P, NT + 1], F32)
+        dd = const.tile([P, TPP], F32)
+        ad = const.tile([P, TPP], F32)
+        ef = const.tile([P, 2, TPP], F32)
+        r1 = const.tile([P, 2, TPP], F32)
+        cf = const.tile([P, 2, TPP, NPIECE], BF16)
+        cmix = const.tile([P, NPIECE], BF16)
+        junk = const.tile([P, D], BF16)
+        sall = const.tile([P, NT, D], BF16)
+        ylow = const.tile([P, TPP // 2, D], BF16)
+        yhigh = wprep.tile([P, TPP // 2, D], BF16, offset=0)
+        acc = psa.tile([P, HALF], F32)
+
+        def ysl(u, v):
+            lim = TPP // 2
+            return ylow[:, u:v, :] if v <= lim else yhigh[:, u - lim : v - lim, :]
 
         def prep_w(j):
-            tp = pst.tile([P, 4, P], F32, tag="tp")
+            tp = psm.tile([P, HALF], F32, tag="mm")
             for c in range(4):
-                nc.tensor.transpose(tp[:, c, :], wrf[:, j * HALF + c * P : j * HALF + (c + 1) * P], ident[:])
-            dst = wgf[:, :, j * P : (j + 1) * P, :]
-            src = tp[:].rearrange("p (g u) r -> p g r u", u=2)
-            if j % 2 == 0:
+                nc.tensor.transpose(tp[:, c * P : (c + 1) * P], wrf[:, j * HALF + c * P : j * HALF + (c + 1) * P], ident[:])
+            wgf = wg[j // 4][:].bitcast(F32).rearrange("p (g r u) -> p g r u", g=2, u=2)
+            dst = wgf[:, :, (j % 4) * P : (j % 4 + 1) * P, :]
+            src = tp[:].rearrange("p (g u r) -> p g r u", g=2, u=2)
+            if j % 4 != 3:
                 nc.scalar.copy(out=dst, in_=src)
             else:
                 nc.vector.tensor_copy(out=dst, in_=src)
@@ -117,246 +155,300 @@ def tile_dispatcher_pa_t_kernel(tc, inv, Wk, bk, out):
                 nc.vector.quantize_mx(
                     out=wc[:, lo : lo + HALF].bitcast(FP8X4),
                     scales=ws[:, lo : lo + HALF],
-                    in_=wg[:, lo * 4 : (lo + HALF) * 4],
+                    in_=wg[h][:, g * 2 * D : (g + 1) * 2 * D],
                 )
-
-        sacc = const.tile([P, 2 * NT], F32)
-        nsq = const.tile([P, NT], F32)
-
-        stot = const.tile([P, NT], F32)
-        nrm = const.tile([P, NT], F32)
-        ncl = const.tile([P, NT], F32)
-        rn = const.tile([P, NT], F32)
-        rr = const.tile([P, NT], F32)
-        ar = const.tile([P, NT], F32)
-        dd = const.tile([P, TPP], F32)
-        ad = const.tile([P, TPP], F32)
-        ef = const.tile([P, 2, TPP], F32)
-        r1 = const.tile([P, 2, TPP], F32)
-        cf = const.tile([P, 2, TPP, NPIECE], BF16)
-        junk = const.tile([P, D], BF16)
-        yall = const.tile([P, TPP, D], BF16)
-        acc = psa.tile([P, HALF], F32)
 
         tps = {}
         grp = {}
         cods = {}
         mmt = {}
-        signs = {}
+        outs = {}
 
-        def stage_t(k):
-            got = []
-            for t in GROUPS[k]:
+        def stage_t(k, a):
+            if k < NG:
                 tp = pst.tile([P, 4, P], F32, tag="tp")
-                src = words(t)
+                src = words(2 * k + a)
                 for c in range(4):
                     nc.tensor.transpose(tp[:, c, :], src[:, c * P : (c + 1) * P], ident[:])
-                got.append(tp)
-            tps[k] = got
+                tps[k, a] = tp
 
         def stage_ev(k, a):
-            n = len(GROUPS[k])
-            if a == 0:
-                gt = gpool.tile([P, n * D], BF16, tag="grp", align_bytes=64)
-                grp[k] = gt
-            if a < n:
-                gf = grp[k][:].bitcast(F32).rearrange("p (a g r u) -> p a g r u", a=n, g=2, u=2)
-                view = tps[k][a][:].rearrange("p (g u) r -> p g r u", u=2)
-                nc.scalar.copy(out=gf[:, a], in_=view)
+            if k < NG:
+                if a == 0:
+                    gt = gpool.tile([P, 2 * D], BF16, tag="grp", align_bytes=64)
+                    grp[k] = gt
+                gf = grp[k][:].bitcast(F32).rearrange("p (a g r u) -> p a g r u", a=2, g=2, u=2)
+                nc.scalar.copy(out=gf[:, a], in_=tps[k, a][:].rearrange("p (g u) r -> p g r u", u=2))
 
         def stage_q(k):
-            n = len(GROUPS[k])
-            cod = cpool.tile([P, n * 256], U32, tag="cod", align_bytes=64)
-            scl = cpool.tile([P, n * 256], U8, tag="scl", align_bytes=64)
-            nc.vector.quantize_mx(out=cod[:].bitcast(FP8X4), scales=scl[:], in_=grp[k][:])
-            cods[k] = (cod, scl)
+            if k < NG:
+                cod = cpool.tile([P, 512], U32, tag="cod", align_bytes=64)
+                scl = cpool.tile([P, 512], U8, tag="scl", align_bytes=64)
+                nc.vector.quantize_mx(out=cod[:].bitcast(FP8X4), scales=scl[:], in_=grp[k][:])
+                cods[k] = (cod, scl)
 
-        def stage_m(k):
-            cod, scl = cods[k]
-            got = []
-            for a in range(len(GROUPS[k])):
-                for h in range(2):
-                    mm = psm.tile([P, HALF], F32, tag="mm")
-                    for g in range(2):
-                        off = (a * 2 + g) * P
-                        lo = g * D + h * HALF
-                        nc.tensor.matmul_mx(
-                            out=mm[:],
-                            lhsT=cod[:, off : off + P].bitcast(FP8X4),
-                            lhsT_scale=scl[:, off : off + P],
-                            rhs=wc[:, lo : lo + HALF].bitcast(FP8X4),
-                            rhs_scale=ws[:, lo : lo + HALF],
-                            start=(g == 0),
-                            stop=(g == 1),
-                        )
-                    got.append(mm)
-            mmt[k] = got
+        def stage_m(k, a, h):
+            if k < NG:
+                cod, scl = cods[k]
+                mm = psm.tile([P, HALF], F32, tag="mm")
+                for g in range(2):
+                    off = (a * 2 + g) * P
+                    lo = g * D + h * HALF
+                    nc.tensor.matmul_mx(
+                        out=mm[:],
+                        lhsT=cod[:, off : off + P].bitcast(FP8X4),
+                        lhsT_scale=scl[:, off : off + P],
+                        rhs=wc[:, lo : lo + HALF].bitcast(FP8X4),
+                        rhs_scale=ws[:, lo : lo + HALF],
+                        start=(g == 0),
+                        stop=(g == 1),
+                    )
+                mmt[k, a, h] = mm
 
-        def stage_e(k):
-            outs = {}
-            for a, t in enumerate(GROUPS[k]):
+        def stage_add(k, a, h):
+            t = 2 * k + a
+            if t not in outs:
                 o = opool.tile([P, D], F32, tag="o")
-                for h in range(2):
-                    nc.vector.scalar_tensor_tensor(
-                        out=o[:, h * HALF : (h + 1) * HALF],
-                        in0=mmt[k][2 * a + h][:],
-                        scalar=1.0,
-                        in1=bias[:, h * HALF : (h + 1) * HALF],
-                        op0=ALU.mult,
-                        op1=ALU.add,
-                        accum_out=sacc[:, h * NT + t : h * NT + t + 1],
-                    )
-                trickle()
-                nc.scalar.activation(out=junk[:], in_=o[:], func=ACT.Square, accum_out=nsq[:, t : t + 1])
                 outs[t] = o
-            for t in GROUPS[k]:
-                sg = spool.tile([P, D], BF16, tag="sg")
-                if t % 2 == 0:
-                    nc.vector.tensor_scalar(
-                        out=sg[:], in0=outs[t][:], scalar1=SIGN_MAG, scalar2=-SIGN_MAG, op0=ALU.min, op1=ALU.max
-                    )
-                else:
-                    nc.scalar.activation(out=sg[:], in_=outs[t][:], func=ACT.Sign)
-                signs[t] = sg
+            nc.vector.scalar_tensor_tensor(
+                out=outs[t][:, h * HALF : (h + 1) * HALF],
+                in0=mmt[k, a, h][:],
+                scalar=1.0,
+                in1=bias[:, h * HALF : (h + 1) * HALF],
+                op0=ALU.mult,
+                op1=ALU.add,
+                accum_out=sacc[:, h * NT + t : h * NT + t + 1],
+            )
 
-        def stage_p(k):
-            for pair in (2 * k - 1, 2 * k):
-                if 0 <= pair < TPP:
-                    nc.vector.tensor_tensor(
-                        out=yall[:, pair, :], in0=signs[pair][:], in1=signs[pair + 1][:], op=ALU.mult
-                    )
-                    trickle()
+        def stage_square(t):
+            nc.scalar.activation(out=junk[:], in_=outs[t][:], func=ACT.Square, accum_out=nsq[:, t : t + 1])
 
-        pending = []
+        def sign_vector(t):
+            nc.vector.tensor_scalar(
+                out=sall[:, t, :], in0=outs[t][:], scalar1=SIGN_MAG, scalar2=-SIGN_MAG, op0=ALU.min, op1=ALU.max
+            )
+
+        def sign_scalar(t):
+            nc.scalar.activation(out=sall[:, t, :], in_=outs[t][:], func=ACT.Sign)
+
+        def products(u, v):
+            nc.vector.tensor_tensor(
+                out=ysl(u, v), in0=sall[:, u:v, :], in1=sall[:, u + 1 : v + 1, :], op=ALU.mult
+            )
+
+        def magnitude(cols):
+            nc.vector.scalar_tensor_tensor(
+                out=ar[:, cols], in0=rr[:, cols], scalar=-1.0, in1=rr[:, cols], op0=ALU.mult, op1=ALU.max
+            )
+
+        def fresh(b):
+            lo, hi = BATCHES[b]
+            return slice(lo if b == 0 else lo + 1, min(hi + 1, NT))
+
+        def stage_norm(b):
+            new = fresh(b)
+            nc.scalar.activation(out=nrm[:, new], in_=nsq[:, new], func=ACT.Sqrt)
 
         def chain(b):
             lo, hi = BATCHES[b]
-            new = slice(lo if b == 0 else lo + 1, hi + 1)
+            new = fresh(b)
             cur = slice(lo, hi)
             nxt = slice(lo + 1, hi + 1)
             v = nc.vector
-            return [
-                lambda: nc.scalar.activation(out=nrm[:, new], in_=nsq[:, new], func=ACT.Sqrt),
-                lambda: v.tensor_tensor(out=stot[:, new], in0=sacc[:, new], in1=sacc[:, NT + new.start : NT + new.stop], op=ALU.add),
-                lambda: v.tensor_scalar(out=ncl[:, new], in0=nrm[:, new], scalar1=1e-8, scalar2=None, op0=ALU.max),
-                lambda: v.reciprocal(out=rn[:, new], in_=ncl[:, new]),
-                lambda: v.tensor_tensor(out=rr[:, new], in0=stot[:, new], in1=rn[:, new], op=ALU.mult),
+            steps = [
+                lambda: v.tensor_tensor(
+                    out=stot[:, new], in0=sacc[:, new], in1=sacc[:, NT + new.start : NT + new.stop], op=ALU.add
+                ),
+                lambda: v.reciprocal(out=rn[:, new], in_=nrm[:, new]),
                 lambda: v.scalar_tensor_tensor(
-                    out=ar[:, new], in0=rr[:, new], scalar=-1.0, in1=rr[:, new], op0=ALU.mult, op1=ALU.max
+                    out=rr[:, new], in0=rn[:, new], scalar=1e8, in1=stot[:, new], op0=ALU.min, op1=ALU.mult
                 ),
                 lambda: v.tensor_tensor(out=dd[:, cur], in0=rr[:, nxt], in1=rr[:, cur], op=ALU.subtract),
-                lambda: v.tensor_tensor(out=ef[:, 1, cur], in0=ar[:, nxt], in1=ar[:, cur], op=ALU.max),
+                lambda: magnitude(new),
                 lambda: v.scalar_tensor_tensor(
                     out=ad[:, cur], in0=dd[:, cur], scalar=-1.0, in1=dd[:, cur], op0=ALU.mult, op1=ALU.max
                 ),
+                lambda: v.tensor_tensor(out=ef[:, 1, cur], in0=ar[:, nxt], in1=ar[:, cur], op=ALU.max),
                 lambda: v.tensor_tensor(out=ef[:, 0, cur], in0=ad[:, cur], in1=ef[:, 1, cur], op=ALU.subtract),
                 lambda: v.tensor_copy(out=cf[:, :, cur, 0], in_=ef[:, :, cur]),
                 lambda: v.tensor_tensor(out=cf[:, :, cur, 1], in0=ef[:, :, cur], in1=cf[:, :, cur, 0], op=ALU.subtract),
                 lambda: v.tensor_tensor(out=r1[:, :, cur], in0=ef[:, :, cur], in1=cf[:, :, cur, 0], op=ALU.subtract),
                 lambda: v.tensor_tensor(out=cf[:, :, cur, 2], in0=r1[:, :, cur], in1=cf[:, :, cur, 1], op=ALU.subtract),
             ]
+            if b == 0:
+                wrap = slice(NT, NT + 1)
+                steps += [
+                    lambda: nc.tensor.matmul(
+                        out=acc[:, RCOL : RCOL + 1], lhsT=shift[:], rhs=rr[:, 0:1], start=True, stop=True
+                    ),
+                    lambda: v.tensor_copy(out=rr[:, wrap], in_=acc[:, RCOL : RCOL + 1]),
+                    lambda: magnitude(wrap),
+                ]
+            return steps
 
-        def trickle(n=1):
-            for _ in range(n):
-                if pending:
-                    pending.pop(0)()
-
-        def weigh(b, part):
+        def weigh(b):
             lo, hi = BATCHES[b]
-            for j in range(4 * part, 4 * part + 4):
+
+            def block(j):
                 col = (b * 8 + j) * NPIECE
                 for pair in range(lo, hi):
                     nc.tensor.matmul(
                         out=acc[:, col : col + NPIECE],
-                        lhsT=yall[:, pair, j * P : (j + 1) * P],
-                        rhs=cf[:, 0, pair, :],
+                        lhsT=ysl(pair, pair + 1)[:, 0, j * P : (j + 1) * P],
+                        rhs=cmix[:] if pair == NT - 3 else cf[:, 0, pair, :],
                         start=(pair == lo),
                         stop=(pair == hi - 1),
                     )
-            if part == 1:
+
+            def constant(u, v, stationary):
                 nc.tensor.matmul(
-                    out=acc[:, YCOLS + lo * NPIECE : YCOLS + hi * NPIECE],
-                    lhsT=ones[:],
-                    rhs=cf[:, 1, lo:hi, :].rearrange("p t c -> p (t c)"),
+                    out=acc[:, YCOLS + u * NPIECE : YCOLS + v * NPIECE],
+                    lhsT=stationary[:],
+                    rhs=cf[:, 1, u:v, :].rearrange("p t c -> p (t c)"),
                     start=True,
                     stop=True,
                 )
 
-        for h in range(2):
-            bb = psm.tile([P, HALF], F32, tag="mm")
-            nc.tensor.matmul(
-                out=bb[:], lhsT=unit[:], rhs=brow[:, h * HALF : (h + 1) * HALF], start=True, stop=True
-            )
-            nc.scalar.copy(out=bias[:, h * HALF : (h + 1) * HALF], in_=bb[:])
-        for j in range(4):
-            prep_w(j)
-        quant_w(0)
-        for j in range(4, 8):
-            prep_w(j)
-        stage_t(0)
-        quant_w(1)
+            steps = [lambda j=j: block(j) for j in range(8)]
+            steps.append(lambda: constant(lo, min(hi, TPP - 1), ones))
+            if hi == TPP:
+                steps.append(lambda: constant(TPP - 1, TPP, most))
+            return steps
+
+        vq = []
+        pq = []
+
+        def trickle(queue, n):
+            for _ in range(min(n, len(queue))):
+                queue.pop(0)()
+
+        dummy = psm.tile([P, HALF], F32, tag="mm")
+        for _ in range(WARMUP):
+            nc.tensor.matmul(out=dummy[:], lhsT=unit[:, 0:P], rhs=unit[:], start=True, stop=True)
+        stage_t(0, 0)
+        stage_t(0, 1)
         stage_ev(0, 0)
         stage_ev(0, 1)
         stage_q(0)
-        stage_t(1)
-        stage_ev(1, 0)
-        stage_ev(1, 1)
-        stage_m(0)
+        for j in range(4):
+            prep_w(j)
+        quant_w(0)
+        bb = psm.tile([P, 8, P], BF16, tag="mm")
+        for c in range(8):
+            nc.tensor.transpose(bb[:, c, :], bcol[:, c : c + 1].to_broadcast([P, P]), identb[:])
+        for j in range(4, 8):
+            prep_w(j)
+        nc.scalar.copy(out=bias[:].rearrange("p (r c) -> p r c", c=8), in_=bb[:].rearrange("p c r -> p r c"))
+        stage_m(0, 0, 0)
+        stage_m(0, 1, 0)
+        quant_w(1)
+        for a in range(2):
+            stage_t(1, a)
+            stage_ev(1, a)
+        stage_add(0, 0, 0)
+        stage_add(0, 1, 0)
         stage_q(1)
-        stage_t(2)
+        stage_m(0, 0, 1)
+        stage_m(0, 1, 1)
+        for a in range(2):
+            stage_t(2, a)
+            stage_ev(2, a)
+        stage_m(1, 0, 0)
+        for a in range(2):
+            stage_t(3, a)
 
-        for k in range(NG + 7):
+        for k in range(NG):
             if k % 2 == 0 and k // 2 + 4 < 8:
-                load_x(k // 2 + 4, 1)
-            if k == 8:
-                nc.sync.dma_start(out=xlast[0 : P - 1, :], in_=xv[1:P, 0, :])
-                nc.sync.dma_start(out=xlast[P - 1 : P, :], in_=flat[TOKENS - 1 : TOKENS, :])
-            if k + 2 < NG:
-                stage_ev(k + 2, 0)
-                stage_ev(k + 2, 1)
-            if k < NG:
-                stage_e(k)
-            if k + 1 < NG:
-                stage_m(k + 1)
-            if k + 3 < NG:
-                stage_t(k + 3)
-            if 1 <= k <= NG:
-                stage_p(k - 1)
-            if k + 2 < NG:
-                stage_q(k + 2)
-            for b, (lo, hi) in enumerate(BATCHES):
+                load_x(k // 2 + 4, 0, 4)
+            for b, (lo, hi) in enumerate(BATCHES[:-1]):
                 if k == hi // 2 + 1:
-                    pending.extend(chain(b))
-                if k == NG:
-                    trickle(len(pending))
-                if k == hi // 2 + 5:
-                    weigh(b, 0)
-                if k == hi // 2 + 6:
-                    weigh(b, 1)
+                    vq.extend(chain(b))
+                if k == hi // 2 + 4:
+                    pq.extend(weigh(b))
+            if k > 0:
+                stage_add(k, 0, 0)
+            stage_ev(k + 3, 0)
+            stage_m(k + 1, 0, 1)
+            stage_add(k, 0, 1)
+            stage_m(k + 1, 1, 0)
+            stage_t(k + 4, 0)
+            stage_square(2 * k)
+            trickle(vq, 3 if k >= NG - 2 else 1)
+            stage_q(k + 2)
+            trickle(vq, 3 if k >= NG - 2 else 1)
+            if k < NG - 1:
+                sign_vector(2 * k)
+            else:
+                sign_scalar(2 * k)
+            trickle(vq, 3 if k >= NG - 2 else 1)
+            if k > 0:
+                stage_add(k, 1, 0)
+            stage_ev(k + 3, 1)
+            for b, (lo, hi) in enumerate(BATCHES[:-1]):
+                if 2 * k == hi:
+                    stage_norm(b)
+            stage_m(k + 1, 1, 1)
+            trickle(pq, 2)
+            stage_t(k + 4, 1)
+            stage_add(k, 1, 1)
+            stage_m(k + 2, 0, 0)
+            trickle(vq, 3 if k >= NG - 2 else 1)
+            if k >= 1:
+                products(2 * k - 2, 2 * k)
+            trickle(vq, 3 if k >= NG - 2 else 1)
+            stage_square(2 * k + 1)
+            if k < NG - 1:
+                sign_scalar(2 * k + 1)
+            trickle(pq, 2)
+
+        stage_norm(NB - 1)
+        sign_vector(NT - 1)
+        products(NT - 2, NT - 1)
+        trickle(vq, len(vq))
+        shifted = const.tile([P, D], BF16)
+        for h in range(2):
+            cols = slice(h * HALF, (h + 1) * HALF)
+            mm = psm.tile([P, HALF], F32, tag="mm")
+            nc.tensor.matmul(out=mm[:], lhsT=shiftb[:], rhs=sall[:, 0, cols], start=True, stop=True)
+            nc.scalar.activation(out=shifted[:, cols], in_=mm[:], func=ACT.Copy, scale=1.0 / SIGN_MAG)
+        pq.extend(weigh(NB - 3))
+        pq.extend(weigh(NB - 2))
+        trickle(pq, len(pq))
+        cool = psm.tile([P, HALF], F32, tag="mm")
+        for _ in range(COOL):
+            nc.tensor.matmul(out=cool[:], lhsT=unit[:, 0:P], rhs=unit[:], start=True, stop=True)
+        last = chain(NB - 1)
+        trickle(last, 6)
+        nc.vector.tensor_tensor(out=yhigh[:, TPP // 2 - 1, :], in0=shifted[:], in1=sall[:, NT - 1, :], op=ALU.mult)
+        trickle(last, len(last))
+        nc.vector.tensor_scalar(out=cmix[:], in0=cf[:, 0, NT - 3, :], scalar1=SIGN_MAG, scalar2=None, op0=ALU.mult)
+        pq.extend(weigh(NB - 1))
+        trickle(pq, len(pq))
 
         accy = acc[:, 0:YCOLS].rearrange("p (b j c) -> p j b c", b=NB, j=8, c=NPIECE)
         ysum = const.tile([P, 8], F32)
         cs = const.tile([P, 1], F32)
-        rep = const.tile([P, 8, P], F32)
+        base = const.tile([P, 1], F32)
         res = const.tile([P, D], F32)
         nc.vector.tensor_reduce(out=ysum[:], in_=accy, axis=AX.XY, op=ALU.add)
         nc.vector.tensor_reduce(out=cs[:], in_=acc[:, YCOLS : YCOLS + TPP * NPIECE], axis=AX.X, op=ALU.add)
-        bcs = []
+        nc.vector.tensor_scalar(out=base[:], in0=cs[:], scalar1=1.0 / 32.0, scalar2=None, op0=ALU.mult)
         for h in range(2):
-            nc.vector.tensor_scalar(
-                out=rep[:, 4 * h : 4 * h + 4, :],
-                in0=ysum[:, 4 * h : 4 * h + 4].unsqueeze(2).to_broadcast([P, 4, P]),
-                scalar1=cs[:, 0:1],
-                scalar2=1.0 / (32.0 * SIGN_MAG),
-                op0=ALU.add,
-                op1=ALU.mult,
-            )
             bc = psm.tile([P, HALF], F32, tag="mm")
             for jj in range(4):
-                nc.tensor.transpose(bc[:, jj * P : (jj + 1) * P], rep[:, 4 * h + jj, :], ident[:])
-            bcs.append(bc)
-        nc.vector.tensor_copy(out=res[:, 0:HALF], in_=bcs[0][:])
-        nc.scalar.copy(out=res[:, HALF:D], in_=bcs[1][:])
+                col = 4 * h + jj
+                nc.tensor.transpose(
+                    bc[:, jj * P : (jj + 1) * P], ysum[:, col : col + 1].to_broadcast([P, P]), ident[:]
+                )
+            cols = slice(h * HALF, (h + 1) * HALF)
+            if h == 0:
+                nc.vector.tensor_scalar(
+                    out=res[:, cols], in0=bc[:], scalar1=1.0 / (32.0 * SIGN_MAG), scalar2=base[:, 0:1], op0=ALU.mult, op1=ALU.add
+                )
+            else:
+                nc.scalar.activation(
+                    out=res[:, cols], in_=bc[:], func=ACT.Identity, scale=1.0 / (32.0 * SIGN_MAG), bias=base[:, 0:1]
+                )
         for h in range(2):
             eng = nc.sync if h == 0 else nc.scalar
             for eb in range(8):

@@ -21,14 +21,16 @@ NG = NT // 2
 HALF = 512
 FLOPS = 2 * TOKENS * D * D
 
-BATCHES = [(0, 8), (8, 16), (16, 24), (24, 28), (28, 32)]
+BATCHES = [(0, 14), (14, 26), (26, 32)]
 NB = len(BATCHES)
 NPIECE = 3
 YCOLS = NB * 8 * NPIECE
 RCOL = 256
-SIGN_MAG = 2.0 ** -64
+YLOW = 17
+SIGN_MAG = 0.5
+VCOLS = 768
 WARMUP = 4
-COOL = 8
+COOL = 4
 PARTS = [(0, 0), (0, 1), (1, 0), (1, 1)]
 
 
@@ -126,16 +128,14 @@ def tile_dispatcher_pa_t_kernel(tc, inv, Wk, bk, out):
         ef = const.tile([P, 2, TPP], F32)
         r1 = const.tile([P, 2, TPP], F32)
         cf = const.tile([P, 2, TPP, NPIECE], BF16)
-        cmix = const.tile([P, NPIECE], BF16)
         junk = const.tile([P, D], BF16)
         sall = const.tile([P, NT, D], BF16)
-        ylow = const.tile([P, TPP // 2, D], BF16)
-        yhigh = wprep.tile([P, TPP // 2, D], BF16, offset=0)
+        ylow = const.tile([P, YLOW, D], BF16)
+        yhigh = wprep.tile([P, TPP - YLOW, D], BF16, offset=0)
         acc = psa.tile([P, HALF], F32)
 
         def ysl(u, v):
-            lim = TPP // 2
-            return ylow[:, u:v, :] if v <= lim else yhigh[:, u - lim : v - lim, :]
+            return ylow[:, u:v, :] if v <= YLOW else yhigh[:, u - YLOW : v - YLOW, :]
 
         def prep_w(j):
             tp = psm.tile([P, HALF], F32, tag="mm")
@@ -144,7 +144,7 @@ def tile_dispatcher_pa_t_kernel(tc, inv, Wk, bk, out):
             wgf = wg[j // 4][:].bitcast(F32).rearrange("p (g r u) -> p g r u", g=2, u=2)
             dst = wgf[:, :, (j % 4) * P : (j % 4 + 1) * P, :]
             src = tp[:].rearrange("p (g u r) -> p g r u", g=2, u=2)
-            if j % 4 != 3:
+            if j not in (2, 3, 7):
                 nc.scalar.copy(out=dst, in_=src)
             else:
                 nc.vector.tensor_copy(out=dst, in_=src)
@@ -223,13 +223,13 @@ def tile_dispatcher_pa_t_kernel(tc, inv, Wk, bk, out):
         def stage_square(t):
             nc.scalar.activation(out=junk[:], in_=outs[t][:], func=ACT.Square, accum_out=nsq[:, t : t + 1])
 
-        def sign_vector(t):
+        def sign_vector(t, n=D):
             nc.vector.tensor_scalar(
-                out=sall[:, t, :], in0=outs[t][:], scalar1=SIGN_MAG, scalar2=-SIGN_MAG, op0=ALU.min, op1=ALU.max
+                out=sall[:, t, 0:n], in0=outs[t][:, 0:n], scalar1=0.0, scalar2=SIGN_MAG, op0=ALU.is_ge, op1=ALU.subtract
             )
 
-        def sign_scalar(t):
-            nc.scalar.activation(out=sall[:, t, :], in_=outs[t][:], func=ACT.Sign)
+        def sign_scalar(t, u=0):
+            nc.scalar.activation(out=sall[:, t, u:D], in_=outs[t][:, u:D], func=ACT.Sign)
 
         def products(u, v):
             nc.vector.tensor_tensor(
@@ -247,6 +247,7 @@ def tile_dispatcher_pa_t_kernel(tc, inv, Wk, bk, out):
 
         def stage_norm(b):
             new = fresh(b)
+            new = slice(new.start, min(new.stop, NT - 1))
             nc.scalar.activation(out=nrm[:, new], in_=nsq[:, new], func=ACT.Sqrt)
 
         def chain(b):
@@ -271,20 +272,27 @@ def tile_dispatcher_pa_t_kernel(tc, inv, Wk, bk, out):
                 lambda: v.tensor_tensor(out=ef[:, 1, cur], in0=ar[:, nxt], in1=ar[:, cur], op=ALU.max),
                 lambda: v.tensor_tensor(out=ef[:, 0, cur], in0=ad[:, cur], in1=ef[:, 1, cur], op=ALU.subtract),
                 lambda: v.tensor_copy(out=cf[:, :, cur, 0], in_=ef[:, :, cur]),
-                lambda: v.tensor_tensor(out=cf[:, :, cur, 1], in0=ef[:, :, cur], in1=cf[:, :, cur, 0], op=ALU.subtract),
                 lambda: v.tensor_tensor(out=r1[:, :, cur], in0=ef[:, :, cur], in1=cf[:, :, cur, 0], op=ALU.subtract),
+                lambda: v.tensor_tensor(out=cf[:, :, cur, 1], in0=ef[:, :, cur], in1=cf[:, :, cur, 0], op=ALU.subtract),
                 lambda: v.tensor_tensor(out=cf[:, :, cur, 2], in0=r1[:, :, cur], in1=cf[:, :, cur, 1], op=ALU.subtract),
             ]
-            if b == 0:
-                wrap = slice(NT, NT + 1)
-                steps += [
-                    lambda: nc.tensor.matmul(
-                        out=acc[:, RCOL : RCOL + 1], lhsT=shift[:], rhs=rr[:, 0:1], start=True, stop=True
+            if hi == TPP:
+                pair = slice(NT - 2, NT - 1)
+                steps.insert(
+                    8,
+                    lambda: v.tensor_scalar(
+                        out=ef[:, 0, pair], in0=ef[:, 0, pair], scalar1=1.0 / SIGN_MAG, scalar2=None, op0=ALU.mult
                     ),
-                    lambda: v.tensor_copy(out=rr[:, wrap], in_=acc[:, RCOL : RCOL + 1]),
-                    lambda: magnitude(wrap),
-                ]
+                )
             return steps
+
+        def wrap_factor():
+            nc.tensor.matmul(out=acc[:, RCOL : RCOL + 1], lhsT=shift[:], rhs=rr[:, 0:1], start=True, stop=True)
+
+        def wrap_magnitude():
+            wrap = slice(NT, NT + 1)
+            nc.vector.tensor_copy(out=rr[:, wrap], in_=acc[:, RCOL : RCOL + 1])
+            magnitude(wrap)
 
         def weigh(b):
             lo, hi = BATCHES[b]
@@ -295,7 +303,7 @@ def tile_dispatcher_pa_t_kernel(tc, inv, Wk, bk, out):
                     nc.tensor.matmul(
                         out=acc[:, col : col + NPIECE],
                         lhsT=ysl(pair, pair + 1)[:, 0, j * P : (j + 1) * P],
-                        rhs=cmix[:] if pair == NT - 3 else cf[:, 0, pair, :],
+                        rhs=cf[:, 0, pair, :],
                         start=(pair == lo),
                         stop=(pair == hi - 1),
                     )
@@ -363,8 +371,10 @@ def tile_dispatcher_pa_t_kernel(tc, inv, Wk, bk, out):
             for b, (lo, hi) in enumerate(BATCHES[:-1]):
                 if k == hi // 2 + 1:
                     vq.extend(chain(b))
-                if k == hi // 2 + 4:
+                if k == hi // 2 + (4 if b == 0 else 2):
                     pq.extend(weigh(b))
+                    if b == 0:
+                        pq.append(wrap_factor)
             if k > 0:
                 stage_add(k, 0, 0)
             stage_ev(k + 3, 0)
@@ -376,10 +386,7 @@ def tile_dispatcher_pa_t_kernel(tc, inv, Wk, bk, out):
             trickle(vq, 3 if k >= NG - 2 else 1)
             stage_q(k + 2)
             trickle(vq, 3 if k >= NG - 2 else 1)
-            if k < NG - 1:
-                sign_vector(2 * k)
-            else:
-                sign_scalar(2 * k)
+            sign_vector(2 * k, VCOLS)
             trickle(vq, 3 if k >= NG - 2 else 1)
             if k > 0:
                 stage_add(k, 1, 0)
@@ -393,35 +400,60 @@ def tile_dispatcher_pa_t_kernel(tc, inv, Wk, bk, out):
             stage_add(k, 1, 1)
             stage_m(k + 2, 0, 0)
             trickle(vq, 3 if k >= NG - 2 else 1)
+            if k == NG - 2:
+                wrap_magnitude()
             if k >= 1:
-                products(2 * k - 2, 2 * k)
+                products(2 * k - 3 if k > 1 else 0, 2 * k - 1)
             trickle(vq, 3 if k >= NG - 2 else 1)
-            stage_square(2 * k + 1)
+            sign_scalar(2 * k, VCOLS)
             if k < NG - 1:
+                stage_square(2 * k + 1)
                 sign_scalar(2 * k + 1)
             trickle(pq, 2)
 
         stage_norm(NB - 1)
-        sign_vector(NT - 1)
-        products(NT - 2, NT - 1)
+        nsqb = const.tile([P, 1], F32)
+        junkb = const.tile([P, HALF], BF16)
+        nc.vector.scalar_tensor_tensor(
+            out=junkb[:],
+            in0=outs[NT - 1][:, HALF:D],
+            scalar=1.0,
+            in1=outs[NT - 1][:, HALF:D],
+            op0=ALU.mult,
+            op1=ALU.mult,
+            accum_out=nsqb[:],
+        )
+        nc.scalar.activation(
+            out=junk[:, 0:HALF], in_=outs[NT - 1][:, 0:HALF], func=ACT.Square, accum_out=nsq[:, NT - 1 : NT]
+        )
+        nc.scalar.activation(
+            out=nrm[:, NT - 1 : NT], in_=nsq[:, NT - 1 : NT], func=ACT.Sqrt, bias=nsqb[:, 0:1]
+        )
         trickle(vq, len(vq))
+        last = chain(NB - 1)
+        trickle(last, 1)
+        sign_vector(NT - 1)
         shifted = const.tile([P, D], BF16)
         for h in range(2):
             cols = slice(h * HALF, (h + 1) * HALF)
             mm = psm.tile([P, HALF], F32, tag="mm")
             nc.tensor.matmul(out=mm[:], lhsT=shiftb[:], rhs=sall[:, 0, cols], start=True, stop=True)
             nc.scalar.activation(out=shifted[:, cols], in_=mm[:], func=ACT.Copy, scale=1.0 / SIGN_MAG)
-        pq.extend(weigh(NB - 3))
-        pq.extend(weigh(NB - 2))
         trickle(pq, len(pq))
         cool = psm.tile([P, HALF], F32, tag="mm")
         for _ in range(COOL):
             nc.tensor.matmul(out=cool[:], lhsT=unit[:, 0:P], rhs=unit[:], start=True, stop=True)
-        last = chain(NB - 1)
-        trickle(last, 6)
-        nc.vector.tensor_tensor(out=yhigh[:, TPP // 2 - 1, :], in0=shifted[:], in1=sall[:, NT - 1, :], op=ALU.mult)
-        trickle(last, len(last))
-        nc.vector.tensor_scalar(out=cmix[:], in0=cf[:, 0, NT - 3, :], scalar1=SIGN_MAG, scalar2=None, op0=ALU.mult)
+
+        def late_product(pair, h):
+            cols = slice(h * HALF, (h + 1) * HALF)
+            following = shifted[:, cols] if pair == NT - 1 else sall[:, pair + 1, cols]
+            nc.vector.tensor_tensor(out=ysl(pair, pair + 1)[:, 0, cols], in0=following, in1=sall[:, pair, cols], op=ALU.mult)
+
+        fillers = [(pair, h) for pair in (NT - 3, NT - 2, NT - 1) for h in range(2)]
+        for n in (1, 1, 2, 2, 1, 1, 1, 2, 1):
+            trickle(last, n)
+            if fillers:
+                late_product(*fillers.pop(0))
         pq.extend(weigh(NB - 1))
         trickle(pq, len(pq))
 
@@ -440,15 +472,17 @@ def tile_dispatcher_pa_t_kernel(tc, inv, Wk, bk, out):
                 nc.tensor.transpose(
                     bc[:, jj * P : (jj + 1) * P], ysum[:, col : col + 1].to_broadcast([P, P]), ident[:]
                 )
-            cols = slice(h * HALF, (h + 1) * HALF)
-            if h == 0:
-                nc.vector.tensor_scalar(
-                    out=res[:, cols], in0=bc[:], scalar1=1.0 / (32.0 * SIGN_MAG), scalar2=base[:, 0:1], op0=ALU.mult, op1=ALU.add
-                )
-            else:
-                nc.scalar.activation(
-                    out=res[:, cols], in_=bc[:], func=ACT.Identity, scale=1.0 / (32.0 * SIGN_MAG), bias=base[:, 0:1]
-                )
+            for u, v in ((0, HALF),) if h == 0 else ((HALF, VCOLS), (VCOLS, D)):
+                scale = 1.0 / (32.0 * (SIGN_MAG if v <= VCOLS else 1.0))
+                spread = bc[:, u - h * HALF : v - h * HALF]
+                if h == 0:
+                    nc.vector.tensor_scalar(
+                        out=res[:, u:v], in0=spread, scalar1=scale, scalar2=base[:, 0:1], op0=ALU.mult, op1=ALU.add
+                    )
+                else:
+                    nc.scalar.activation(
+                        out=res[:, u:v], in_=spread, func=ACT.Identity, scale=scale, bias=base[:, 0:1]
+                    )
         for h in range(2):
             eng = nc.sync if h == 0 else nc.scalar
             for eb in range(8):

@@ -21,15 +21,15 @@ NG = NT // 2
 HALF = 512
 FLOPS = 2 * TOKENS * D * D
 
-BATCHES = [(0, 14), (14, 26), (26, 32)]
+BATCHES = [(0, 13), (13, 27), (27, 32)]
 NB = len(BATCHES)
 NPIECE = 3
 YCOLS = NB * 8 * NPIECE
 RCOL = 256
 YLOW = 17
-SIGN_MAG = 0.5
-VCOLS = 768
-WARMUP = 4
+BIG = 2.0 ** 64
+VCOLS = 896
+WARMUP = 5
 COOL = 4
 PARTS = [(0, 0), (0, 1), (1, 0), (1, 1)]
 
@@ -53,6 +53,7 @@ def tile_dispatcher_pa_t_kernel(tc, inv, Wk, bk, out):
 
         bcol = const.tile([P, 8], BF16)
         nc.scalar.dma_start(out=bcol[:], in_=bk.rearrange("(p c) -> p c", c=8))
+        bbig = const.tile([P, 8], BF16)
         unit = const.tile([P, HALF], BF16)
         nc.vector.memset(unit[:], 1.0)
         ident = const.tile([P, P], F32)
@@ -63,6 +64,7 @@ def tile_dispatcher_pa_t_kernel(tc, inv, Wk, bk, out):
         nc.vector.memset(warm[:], 1.0)
         nc.scalar.activation(out=warm[:, 1:2], in_=warm[:, 0:1], func=ACT.Sqrt)
         bias = const.tile([P, D], BF16)
+        acc = psa.tile([P, HALF], F32)
         identb = const.tile([P, P], BF16)
         nc.vector.tensor_copy(out=identb[:], in_=ident[:])
         shift = const.tile([P, P], F32)
@@ -80,21 +82,23 @@ def tile_dispatcher_pa_t_kernel(tc, inv, Wk, bk, out):
             op1=ALU.add,
         )
 
+        nc.vector.tensor_scalar(out=bbig[:], in0=bcol[:], scalar1=BIG, scalar2=None, op0=ALU.mult)
+
         ctx.enter_context(tc.manual_schedule())
 
         wraw = wprep.tile([P, 8 * D], BF16, offset=0)
-        wleft = wprep.tile([P, 4 * D], BF16, align_bytes=64, offset=16 * D)
-        wright = wprep.tile([P, 4 * D], BF16, align_bytes=64, offset=24 * D)
-        wg = [wleft, wright]
+        wg = {}
+        for i in range(4):
+            part = wprep.tile([P, 2 * D], BF16, align_bytes=64, offset=(16 + 4 * i) * D, name="wg%d" % i)
+            wg[i // 2, i % 2] = part
         wrf = wraw[:].bitcast(F32)
         wc = const.tile([P, 2 * D], U32, align_bytes=64)
         ws = const.tile([P, 2 * D], U8, align_bytes=64)
         xraw = {}
 
-        def load_w(c):
+        def load_w(u, v):
             nc.sync.dma_start(
-                out=wraw[:, c * 2 * D : (c + 1) * 2 * D].rearrange("p (j k) -> p j k", j=2),
-                in_=wv[:, 2 * c : 2 * c + 2, :],
+                out=wraw[:, u * D : v * D].rearrange("p (j k) -> p j k", j=v - u), in_=wv[:, u:v, :]
             )
 
         def load_x(c, u, v):
@@ -106,9 +110,10 @@ def tile_dispatcher_pa_t_kernel(tc, inv, Wk, bk, out):
                 in_=xv[:, 4 * c + u : 4 * c + v, :],
             )
 
-        load_x(0, 0, 2)
-        for c in range(4):
-            load_w(c)
+        load_x(0, 0, 1)
+        for u, v in ((0, 2), (2, 4), (4, 6), (6, 7), (7, 8)):
+            load_w(u, v)
+        load_x(0, 1, 2)
         load_x(0, 2, 4)
         for c in range(1, 4):
             load_x(c, 0, 4)
@@ -119,7 +124,7 @@ def tile_dispatcher_pa_t_kernel(tc, inv, Wk, bk, out):
         sacc = const.tile([P, 2 * NT], F32)
         nsq = const.tile([P, NT], F32)
         stot = const.tile([P, NT], F32)
-        nrm = const.tile([P, NT], F32)
+        rsq = const.tile([P, NT], F32)
         rn = const.tile([P, NT], F32)
         rr = const.tile([P, NT + 1], F32)
         ar = const.tile([P, NT + 1], F32)
@@ -132,30 +137,35 @@ def tile_dispatcher_pa_t_kernel(tc, inv, Wk, bk, out):
         sall = const.tile([P, NT, D], BF16)
         ylow = const.tile([P, YLOW, D], BF16)
         yhigh = wprep.tile([P, TPP - YLOW, D], BF16, offset=0)
-        acc = psa.tile([P, HALF], F32)
 
         def ysl(u, v):
             return ylow[:, u:v, :] if v <= YLOW else yhigh[:, u - YLOW : v - YLOW, :]
 
-        def prep_w(j):
-            tp = psm.tile([P, HALF], F32, tag="mm")
-            for c in range(4):
-                nc.tensor.transpose(tp[:, c * P : (c + 1) * P], wrf[:, j * HALF + c * P : j * HALF + (c + 1) * P], ident[:])
-            wgf = wg[j // 4][:].bitcast(F32).rearrange("p (g r u) -> p g r u", g=2, u=2)
-            dst = wgf[:, :, (j % 4) * P : (j % 4 + 1) * P, :]
-            src = tp[:].rearrange("p (g u r) -> p g r u", g=2, u=2)
-            if j not in (2, 3, 7):
-                nc.scalar.copy(out=dst, in_=src)
-            else:
-                nc.vector.tensor_copy(out=dst, in_=src)
+        def keep_warm(n, u=0):
+            for _ in range(n):
+                nc.tensor.matmul(
+                    out=acc[:, u:HALF], lhsT=unit[:, 0:P], rhs=unit[:, u:HALF], start=True, stop=True
+                )
+
+        def prep_w(u, v):
+            h = u // 4
+            for g in range(2):
+                tp = psm.tile([P, HALF], F32, tag="mm")
+                for j in range(u, v):
+                    for c in range(2):
+                        lo = ((j - u) * 2 + c) * P
+                        at = j * HALF + (2 * g + c) * P
+                        nc.tensor.transpose(tp[:, lo : lo + P], wrf[:, at : at + P], ident[:])
+                dst = wg[h, g][:].bitcast(F32)[:, (u - 4 * h) * 2 * P : (v - 4 * h) * 2 * P]
+                src = tp[:, 0 : (v - u) * 2 * P].rearrange("p (j w r) -> p j r w", j=v - u, w=2)
+                copy = nc.scalar.copy if g == 0 else nc.vector.tensor_copy
+                copy(out=dst.rearrange("p (j r w) -> p j r w", j=v - u, w=2), in_=src)
 
         def quant_w(h):
             for g in range(2):
                 lo = g * D + h * HALF
                 nc.vector.quantize_mx(
-                    out=wc[:, lo : lo + HALF].bitcast(FP8X4),
-                    scales=ws[:, lo : lo + HALF],
-                    in_=wg[h][:, g * 2 * D : (g + 1) * 2 * D],
+                    out=wc[:, lo : lo + HALF].bitcast(FP8X4), scales=ws[:, lo : lo + HALF], in_=wg[h, g][:]
                 )
 
         tps = {}
@@ -172,20 +182,27 @@ def tile_dispatcher_pa_t_kernel(tc, inv, Wk, bk, out):
                     nc.tensor.transpose(tp[:, c, :], src[:, c * P : (c + 1) * P], ident[:])
                 tps[k, a] = tp
 
-        def stage_ev(k, a):
+        def stage_ev(k, a, copy=nc.scalar.copy):
             if k < NG:
                 if a == 0:
                     gt = gpool.tile([P, 2 * D], BF16, tag="grp", align_bytes=64)
                     grp[k] = gt
                 gf = grp[k][:].bitcast(F32).rearrange("p (a g r u) -> p a g r u", a=2, g=2, u=2)
-                nc.scalar.copy(out=gf[:, a], in_=tps[k, a][:].rearrange("p (g u) r -> p g r u", u=2))
+                copy(out=gf[:, a], in_=tps[k, a][:].rearrange("p (g u) r -> p g r u", u=2))
 
-        def stage_q(k):
+        def stage_q(k, part=(0, 2)):
             if k < NG:
-                cod = cpool.tile([P, 512], U32, tag="cod", align_bytes=64)
-                scl = cpool.tile([P, 512], U8, tag="scl", align_bytes=64)
-                nc.vector.quantize_mx(out=cod[:].bitcast(FP8X4), scales=scl[:], in_=grp[k][:])
-                cods[k] = (cod, scl)
+                if part[0] == 0:
+                    cod = cpool.tile([P, 512], U32, tag="cod", align_bytes=64)
+                    scl = cpool.tile([P, 512], U8, tag="scl", align_bytes=64)
+                    cods[k] = (cod, scl)
+                cod, scl = cods[k]
+                u, v = part
+                nc.vector.quantize_mx(
+                    out=cod[:, u * 256 : v * 256].bitcast(FP8X4),
+                    scales=scl[:, u * 256 : v * 256],
+                    in_=grp[k][:, u * D : v * D],
+                )
 
         def stage_m(k, a, h):
             if k < NG:
@@ -213,7 +230,7 @@ def tile_dispatcher_pa_t_kernel(tc, inv, Wk, bk, out):
             nc.vector.scalar_tensor_tensor(
                 out=outs[t][:, h * HALF : (h + 1) * HALF],
                 in0=mmt[k, a, h][:],
-                scalar=1.0,
+                scalar=BIG,
                 in1=bias[:, h * HALF : (h + 1) * HALF],
                 op0=ALU.mult,
                 op1=ALU.add,
@@ -221,15 +238,24 @@ def tile_dispatcher_pa_t_kernel(tc, inv, Wk, bk, out):
             )
 
         def stage_square(t):
-            nc.scalar.activation(out=junk[:], in_=outs[t][:], func=ACT.Square, accum_out=nsq[:, t : t + 1])
+            nc.scalar.activation(out=junk[:], in_=outs[t][:], func=ACT.Square, scale=1.0 / BIG, accum_out=nsq[:, t : t + 1])
 
-        def sign_vector(t, n=D):
+        def sign_vector(t, n):
             nc.vector.tensor_scalar(
-                out=sall[:, t, 0:n], in0=outs[t][:, 0:n], scalar1=0.0, scalar2=SIGN_MAG, op0=ALU.is_ge, op1=ALU.subtract
+                out=sall[:, t, 0:n], in0=outs[t][:, 0:n], scalar1=1.0, scalar2=-1.0, op0=ALU.min, op1=ALU.max
             )
 
         def sign_scalar(t, u=0):
             nc.scalar.activation(out=sall[:, t, u:D], in_=outs[t][:, u:D], func=ACT.Sign)
+
+        shifted = const.tile([P, D], BF16)
+
+        def shift_signs():
+            for h in range(2):
+                cols = slice(h * HALF, (h + 1) * HALF)
+                mm = psm.tile([P, HALF], F32, tag="mm")
+                nc.tensor.matmul(out=mm[:], lhsT=shiftb[:], rhs=sall[:, 0, cols], start=True, stop=True)
+                nc.scalar.copy(out=shifted[:, cols], in_=mm[:])
 
         def products(u, v):
             nc.vector.tensor_tensor(
@@ -245,46 +271,52 @@ def tile_dispatcher_pa_t_kernel(tc, inv, Wk, bk, out):
             lo, hi = BATCHES[b]
             return slice(lo if b == 0 else lo + 1, min(hi + 1, NT))
 
-        def stage_norm(b):
-            new = fresh(b)
-            new = slice(new.start, min(new.stop, NT - 1))
-            nc.scalar.activation(out=nrm[:, new], in_=nsq[:, new], func=ACT.Sqrt)
-
         def chain(b):
             lo, hi = BATCHES[b]
             new = fresh(b)
             cur = slice(lo, hi)
             nxt = slice(lo + 1, hi + 1)
             v = nc.vector
-            steps = [
-                lambda: v.tensor_tensor(
+
+            def total():
+                v.tensor_tensor(
                     out=stot[:, new], in0=sacc[:, new], in1=sacc[:, NT + new.start : NT + new.stop], op=ALU.add
-                ),
-                lambda: v.reciprocal(out=rn[:, new], in_=nrm[:, new]),
-                lambda: v.scalar_tensor_tensor(
-                    out=rr[:, new], in0=rn[:, new], scalar=1e8, in1=stot[:, new], op0=ALU.min, op1=ALU.mult
-                ),
-                lambda: v.tensor_tensor(out=dd[:, cur], in0=rr[:, nxt], in1=rr[:, cur], op=ALU.subtract),
-                lambda: magnitude(new),
-                lambda: v.scalar_tensor_tensor(
-                    out=ad[:, cur], in0=dd[:, cur], scalar=-1.0, in1=dd[:, cur], op0=ALU.mult, op1=ALU.max
-                ),
-                lambda: v.tensor_tensor(out=ef[:, 1, cur], in0=ar[:, nxt], in1=ar[:, cur], op=ALU.max),
-                lambda: v.tensor_tensor(out=ef[:, 0, cur], in0=ad[:, cur], in1=ef[:, 1, cur], op=ALU.subtract),
-                lambda: v.tensor_copy(out=cf[:, :, cur, 0], in_=ef[:, :, cur]),
-                lambda: v.tensor_tensor(out=r1[:, :, cur], in0=ef[:, :, cur], in1=cf[:, :, cur, 0], op=ALU.subtract),
-                lambda: v.tensor_tensor(out=cf[:, :, cur, 1], in0=ef[:, :, cur], in1=cf[:, :, cur, 0], op=ALU.subtract),
-                lambda: v.tensor_tensor(out=cf[:, :, cur, 2], in0=r1[:, :, cur], in1=cf[:, :, cur, 1], op=ALU.subtract),
-            ]
-            if hi == TPP:
-                pair = slice(NT - 2, NT - 1)
-                steps.insert(
-                    8,
-                    lambda: v.tensor_scalar(
-                        out=ef[:, 0, pair], in0=ef[:, 0, pair], scalar1=1.0 / SIGN_MAG, scalar2=None, op0=ALU.mult
-                    ),
                 )
-            return steps
+
+            def factor():
+                v.scalar_tensor_tensor(
+                    out=rr[:, new], in0=rn[:, new], scalar=1e8, in1=stot[:, new], op0=ALU.min, op1=ALU.mult
+                )
+
+            def difference():
+                v.tensor_tensor(out=dd[:, cur], in0=rr[:, nxt], in1=rr[:, cur], op=ALU.subtract)
+                magnitude(new)
+
+            def larger():
+                v.scalar_tensor_tensor(
+                    out=ad[:, cur], in0=dd[:, cur], scalar=-1.0, in1=dd[:, cur], op0=ALU.mult, op1=ALU.max
+                )
+                v.tensor_tensor(out=ef[:, 1, cur], in0=ar[:, nxt], in1=ar[:, cur], op=ALU.max)
+
+            def weight():
+                v.tensor_tensor(out=ef[:, 0, cur], in0=ad[:, cur], in1=ef[:, 1, cur], op=ALU.subtract)
+
+            def first_piece():
+                v.tensor_copy(out=cf[:, :, cur, 0], in_=ef[:, :, cur])
+
+            def second_piece():
+                v.tensor_tensor(out=r1[:, :, cur], in0=ef[:, :, cur], in1=cf[:, :, cur, 0], op=ALU.subtract)
+                v.tensor_tensor(out=cf[:, :, cur, 1], in0=ef[:, :, cur], in1=cf[:, :, cur, 0], op=ALU.subtract)
+
+            def third_piece():
+                v.tensor_tensor(out=cf[:, :, cur, 2], in0=r1[:, :, cur], in1=cf[:, :, cur, 1], op=ALU.subtract)
+
+            return [total, factor, difference, larger, weight, first_piece, second_piece, third_piece]
+
+        def inverse_norm(b):
+            new = fresh(b)
+            nc.vector.reciprocal(out=rsq[:, new], in_=nsq[:, new])
+            nc.scalar.activation(out=rn[:, new], in_=rsq[:, new], func=ACT.Sqrt)
 
         def wrap_factor():
             nc.tensor.matmul(out=acc[:, RCOL : RCOL + 1], lhsT=shift[:], rhs=rr[:, 0:1], start=True, stop=True)
@@ -318,6 +350,9 @@ def tile_dispatcher_pa_t_kernel(tc, inv, Wk, bk, out):
                 )
 
             steps = [lambda j=j: block(j) for j in range(8)]
+            if b == 1:
+                for i in (1, 2, 4, 6):
+                    steps[i : i + 1] = [steps[i], lambda: keep_warm(2, RCOL + 2)]
             steps.append(lambda: constant(lo, min(hi, TPP - 1), ones))
             if hi == TPP:
                 steps.append(lambda: constant(TPP - 1, TPP, most))
@@ -330,163 +365,172 @@ def tile_dispatcher_pa_t_kernel(tc, inv, Wk, bk, out):
             for _ in range(min(n, len(queue))):
                 queue.pop(0)()
 
-        dummy = psm.tile([P, HALF], F32, tag="mm")
-        for _ in range(WARMUP):
-            nc.tensor.matmul(out=dummy[:], lhsT=unit[:, 0:P], rhs=unit[:], start=True, stop=True)
+        keep_warm(WARMUP)
         stage_t(0, 0)
-        stage_t(0, 1)
         stage_ev(0, 0)
-        stage_ev(0, 1)
-        stage_q(0)
-        for j in range(4):
-            prep_w(j)
-        quant_w(0)
-        bb = psm.tile([P, 8, P], BF16, tag="mm")
+        stage_q(0, (0, 1))
+        bb = pst.tile([P, 8, P], BF16, tag="tp")
         for c in range(8):
-            nc.tensor.transpose(bb[:, c, :], bcol[:, c : c + 1].to_broadcast([P, P]), identb[:])
-        for j in range(4, 8):
-            prep_w(j)
+            nc.tensor.transpose(bb[:, c, :], bbig[:, c : c + 1].to_broadcast([P, P]), identb[:])
         nc.scalar.copy(out=bias[:].rearrange("p (r c) -> p r c", c=8), in_=bb[:].rearrange("p c r -> p r c"))
+        keep_warm(1)
+        prep_w(0, 2)
+        keep_warm(2)
+        prep_w(2, 4)
+        keep_warm(2)
+        quant_w(0)
+        prep_w(4, 6)
+        keep_warm(2)
+        prep_w(6, 8)
+        stage_t(0, 1)
+        stage_ev(0, 1)
         stage_m(0, 0, 0)
-        stage_m(0, 1, 0)
         quant_w(1)
-        for a in range(2):
-            stage_t(1, a)
-            stage_ev(1, a)
-        stage_add(0, 0, 0)
-        stage_add(0, 1, 0)
-        stage_q(1)
+        stage_t(1, 0)
+        stage_ev(1, 0)
+        stage_t(1, 1)
+        stage_ev(1, 1)
         stage_m(0, 0, 1)
+        stage_add(0, 0, 0)
+        stage_q(0, (1, 2))
+        stage_add(0, 0, 1)
+        stage_m(0, 1, 0)
         stage_m(0, 1, 1)
-        for a in range(2):
-            stage_t(2, a)
-            stage_ev(2, a)
+        stage_q(1)
+        stage_square(0)
+        stage_t(2, 0)
+        stage_ev(2, 0)
+        stage_t(2, 1)
+        stage_add(0, 1, 0)
+        stage_add(0, 1, 1)
+        stage_ev(2, 1)
         stage_m(1, 0, 0)
-        for a in range(2):
-            stage_t(3, a)
+        stage_t(3, 0)
+        stage_ev(3, 0)
+        stage_t(3, 1)
+        stage_m(1, 0, 1)
+        sign_vector(0, VCOLS)
+        stage_q(2)
+        sign_scalar(0, VCOLS)
+        stage_square(1)
+        stage_m(1, 1, 0)
+        stage_t(4, 0)
+        stage_ev(3, 1)
+        stage_m(1, 1, 1)
+        stage_t(4, 1)
+        sign_scalar(1)
+        stage_m(2, 0, 0)
+        load_x(4, 0, 4)
 
-        for k in range(NG):
+        for k in range(1, NG):
             if k % 2 == 0 and k // 2 + 4 < 8:
                 load_x(k // 2 + 4, 0, 4)
+            share = VCOLS if k < NG - 3 else 0 if k < NG - 1 else D
+            stage_add(k, 0, 0)
+            trickle(vq, 1)
+            stage_ev(k + 3, 0)
+            stage_m(k + 1, 0, 1)
+            stage_add(k, 0, 1)
             for b, (lo, hi) in enumerate(BATCHES[:-1]):
                 if k == hi // 2 + 1:
+                    inverse_norm(b)
                     vq.extend(chain(b))
                 if k == hi // 2 + (4 if b == 0 else 2):
                     pq.extend(weigh(b))
                     if b == 0:
                         pq.append(wrap_factor)
-            if k > 0:
-                stage_add(k, 0, 0)
-            stage_ev(k + 3, 0)
-            stage_m(k + 1, 0, 1)
-            stage_add(k, 0, 1)
             stage_m(k + 1, 1, 0)
             stage_t(k + 4, 0)
             stage_square(2 * k)
-            trickle(vq, 3 if k >= NG - 2 else 1)
             stage_q(k + 2)
-            trickle(vq, 3 if k >= NG - 2 else 1)
-            sign_vector(2 * k, VCOLS)
-            trickle(vq, 3 if k >= NG - 2 else 1)
-            if k > 0:
-                stage_add(k, 1, 0)
+            trickle(vq, 1)
+            if share > 0:
+                sign_vector(2 * k, share)
+                trickle(vq, 1)
+            stage_add(k, 1, 0)
+            trickle(vq, 1)
             stage_ev(k + 3, 1)
-            for b, (lo, hi) in enumerate(BATCHES[:-1]):
-                if 2 * k == hi:
-                    stage_norm(b)
+            if share < D:
+                sign_scalar(2 * k, share)
             stage_m(k + 1, 1, 1)
-            trickle(pq, 2)
+            if k < NG - 1:
+                trickle(pq, 3)
             stage_t(k + 4, 1)
             stage_add(k, 1, 1)
+            trickle(vq, 1)
             stage_m(k + 2, 0, 0)
-            trickle(vq, 3 if k >= NG - 2 else 1)
             if k == NG - 2:
                 wrap_magnitude()
-            if k >= 1:
-                products(2 * k - 3 if k > 1 else 0, 2 * k - 1)
-            trickle(vq, 3 if k >= NG - 2 else 1)
-            sign_scalar(2 * k, VCOLS)
+                shift_signs()
+            products(max(2 * k - 3, 0), 2 * k - 1 if k < NG - 1 else 2 * k)
             if k < NG - 1:
                 stage_square(2 * k + 1)
                 sign_scalar(2 * k + 1)
-            trickle(pq, 2)
+            trickle(pq, 3)
 
-        stage_norm(NB - 1)
-        nsqb = const.tile([P, 1], F32)
-        junkb = const.tile([P, HALF], BF16)
-        nc.vector.scalar_tensor_tensor(
-            out=junkb[:],
-            in0=outs[NT - 1][:, HALF:D],
-            scalar=1.0,
-            in1=outs[NT - 1][:, HALF:D],
-            op0=ALU.mult,
-            op1=ALU.mult,
-            accum_out=nsqb[:],
-        )
-        nc.scalar.activation(
-            out=junk[:, 0:HALF], in_=outs[NT - 1][:, 0:HALF], func=ACT.Square, accum_out=nsq[:, NT - 1 : NT]
-        )
-        nc.scalar.activation(
-            out=nrm[:, NT - 1 : NT], in_=nsq[:, NT - 1 : NT], func=ACT.Sqrt, bias=nsqb[:, 0:1]
-        )
-        trickle(vq, len(vq))
+        stage_square(NT - 1)
+        inverse_norm(NB - 1)
         last = chain(NB - 1)
-        trickle(last, 1)
-        sign_vector(NT - 1)
-        shifted = const.tile([P, D], BF16)
-        for h in range(2):
-            cols = slice(h * HALF, (h + 1) * HALF)
-            mm = psm.tile([P, HALF], F32, tag="mm")
-            nc.tensor.matmul(out=mm[:], lhsT=shiftb[:], rhs=sall[:, 0, cols], start=True, stop=True)
-            nc.scalar.activation(out=shifted[:, cols], in_=mm[:], func=ACT.Copy, scale=1.0 / SIGN_MAG)
+        sign_scalar(NT - 1)
+        trickle(vq, len(vq))
         trickle(pq, len(pq))
-        cool = psm.tile([P, HALF], F32, tag="mm")
-        for _ in range(COOL):
-            nc.tensor.matmul(out=cool[:], lhsT=unit[:, 0:P], rhs=unit[:], start=True, stop=True)
+        keep_warm(COOL, RCOL + 2)
 
         def late_product(pair, h):
             cols = slice(h * HALF, (h + 1) * HALF)
             following = shifted[:, cols] if pair == NT - 1 else sall[:, pair + 1, cols]
             nc.vector.tensor_tensor(out=ysl(pair, pair + 1)[:, 0, cols], in0=following, in1=sall[:, pair, cols], op=ALU.mult)
 
-        fillers = [(pair, h) for pair in (NT - 3, NT - 2, NT - 1) for h in range(2)]
-        for n in (1, 1, 2, 2, 1, 1, 1, 2, 1):
-            trickle(last, n)
-            if fillers:
+        fillers = [(pair, h) for pair in (NT - 2, NT - 1) for h in range(2)]
+        for i in range(len(last)):
+            trickle(last, 1)
+            if i >= 3 and fillers:
                 late_product(*fillers.pop(0))
-        pq.extend(weigh(NB - 1))
-        trickle(pq, len(pq))
-
-        accy = acc[:, 0:YCOLS].rearrange("p (b j c) -> p j b c", b=NB, j=8, c=NPIECE)
-        ysum = const.tile([P, 8], F32)
-        cs = const.tile([P, 1], F32)
         base = const.tile([P, 1], F32)
+        cs = const.tile([P, 1], F32)
+        ysum = const.tile([P, 8], F32)
         res = const.tile([P, D], F32)
-        nc.vector.tensor_reduce(out=ysum[:], in_=accy, axis=AX.XY, op=ALU.add)
-        nc.vector.tensor_reduce(out=cs[:], in_=acc[:, YCOLS : YCOLS + TPP * NPIECE], axis=AX.X, op=ALU.add)
-        nc.vector.tensor_scalar(out=base[:], in0=cs[:], scalar1=1.0 / 32.0, scalar2=None, op0=ALU.mult)
+        accy = acc[:, 0:YCOLS].rearrange("p (b j c) -> p j b c", b=NB, j=8, c=NPIECE)
+        scale = 1.0 / (32.0 * BIG)
+        final = weigh(NB - 1)
+        for step in final[0:4] + final[8:]:
+            step()
         for h in range(2):
-            bc = psm.tile([P, HALF], F32, tag="mm")
-            for jj in range(4):
-                col = 4 * h + jj
-                nc.tensor.transpose(
-                    bc[:, jj * P : (jj + 1) * P], ysum[:, col : col + 1].to_broadcast([P, P]), ident[:]
+            js = slice(4 * h, 4 * h + 4)
+            nc.vector.tensor_reduce(out=ysum[:, js], in_=accy[:, js], axis=AX.XY, op=ALU.add)
+            if h == 0:
+                nc.vector.tensor_reduce(
+                    out=cs[:], in_=acc[:, YCOLS : YCOLS + TPP * NPIECE], axis=AX.X, op=ALU.add
                 )
-            for u, v in ((0, HALF),) if h == 0 else ((HALF, VCOLS), (VCOLS, D)):
-                scale = 1.0 / (32.0 * (SIGN_MAG if v <= VCOLS else 1.0))
-                spread = bc[:, u - h * HALF : v - h * HALF]
-                if h == 0:
-                    nc.vector.tensor_scalar(
-                        out=res[:, u:v], in0=spread, scalar1=scale, scalar2=base[:, 0:1], op0=ALU.mult, op1=ALU.add
+                nc.vector.tensor_scalar(out=base[:], in0=cs[:], scalar1=scale, scalar2=None, op0=ALU.mult)
+            for q in range(2):
+                bc = psm.tile([P, HALF], F32, tag="mm")
+                for i in range(2):
+                    j = 4 * h + 2 * q + i
+                    nc.tensor.transpose(
+                        bc[:, i * P : (i + 1) * P], ysum[:, j : j + 1].to_broadcast([P, P]), ident[:]
+                    )
+                cols = slice((4 * h + 2 * q) * P, (4 * h + 2 * q + 2) * P)
+                if q == 1:
+                    nc.scalar.activation(
+                        out=res[:, cols], in_=bc[:, 0 : 2 * P], func=ACT.Identity, scale=scale, bias=base[:, 0:1]
                     )
                 else:
-                    nc.scalar.activation(
-                        out=res[:, u:v], in_=spread, func=ACT.Identity, scale=scale, bias=base[:, 0:1]
+                    nc.vector.tensor_scalar(
+                        out=res[:, cols],
+                        in0=bc[:, 0 : 2 * P],
+                        scalar1=scale,
+                        scalar2=base[:, 0:1],
+                        op0=ALU.mult,
+                        op1=ALU.add,
                     )
-        for h in range(2):
-            eng = nc.sync if h == 0 else nc.scalar
-            for eb in range(8):
+            for i in range(2):
+                eng = nc.sync if i == 0 else nc.scalar
+                cols = slice(h * HALF, (h + 1) * HALF)
                 eng.dma_start(
-                    out=out[eb * P : (eb + 1) * P, h * HALF : (h + 1) * HALF],
-                    in_=res[:, h * HALF : (h + 1) * HALF],
+                    out=out[4 * i * P : 4 * (i + 1) * P, cols].rearrange("(e p) d -> p e d", p=P),
+                    in_=res[:, cols].unsqueeze(1).to_broadcast([P, 4, HALF]),
                 )
+            if h == 0:
+                for step in final[4:8]:
+                    step()

from contextlib import ExitStack

import concourse.mybir as mybir
from concourse.masks import make_identity

F32 = mybir.dt.float32
BF16 = mybir.dt.bfloat16
U32 = mybir.dt.uint32
U8 = mybir.dt.uint8
FP8X4 = mybir.dt.float8_e4m3fn_x4
ALU = mybir.AluOpType
ACT = mybir.ActivationFunctionType
AX = mybir.AxisListType

P = 128
D = 1024
TOKENS = 4096
TPP = TOKENS // P
NT = TPP
NG = NT // 2
HALF = 512
FLOPS = 2 * TOKENS * D * D

BATCHES = [(0, 13), (13, 27), (27, 32)]
NB = len(BATCHES)
NPIECE = 3
YCOLS = NB * 8 * NPIECE
RCOL = 256
YLOW = 17
BIG = 2.0 ** 64
VCOLS = 896
WARMUP = 5
COOL = 4
PARTS = [(0, 0), (0, 1), (1, 0), (1, 1)]


def tile_dispatcher_pa_t_kernel(tc, inv, Wk, bk, out):
    nc = tc.nc
    flat = inv.flatten_outer_dims()
    xv = flat.rearrange("(p t) k -> p t k", t=TPP)
    wv = Wk.rearrange("(j p) k -> p j k", p=P)

    with ExitStack() as ctx:
        const = ctx.enter_context(tc.tile_pool(name="const", bufs=1))
        wprep = ctx.enter_context(tc.tile_pool(name="wprep", bufs=1))
        xpool = ctx.enter_context(tc.tile_pool(name="xpool", bufs=4))
        gpool = ctx.enter_context(tc.tile_pool(name="gpool", bufs=3))
        cpool = ctx.enter_context(tc.tile_pool(name="cpool", bufs=3))
        opool = ctx.enter_context(tc.tile_pool(name="opool", bufs=5))
        pst = ctx.enter_context(tc.psum_pool(name="pst", bufs=2))
        psm = ctx.enter_context(tc.psum_pool(name="psm", bufs=5))
        psa = ctx.enter_context(tc.psum_pool(name="psa", bufs=1))

        bcol = const.tile([P, 8], BF16)
        nc.scalar.dma_start(out=bcol[:], in_=bk.rearrange("(p c) -> p c", c=8))
        bbig = const.tile([P, 8], BF16)
        unit = const.tile([P, HALF], BF16)
        nc.vector.memset(unit[:], 1.0)
        ident = const.tile([P, P], F32)
        make_identity(nc, ident[:])
        ones = const.tile([P, P], BF16)
        nc.vector.memset(ones[:], 1.0)
        warm = const.tile([P, 2], F32)
        nc.vector.memset(warm[:], 1.0)
        nc.scalar.activation(out=warm[:, 1:2], in_=warm[:, 0:1], func=ACT.Sqrt)
        bias = const.tile([P, D], BF16)
        acc = psa.tile([P, HALF], F32)
        identb = const.tile([P, P], BF16)
        nc.vector.tensor_copy(out=identb[:], in_=ident[:])
        shift = const.tile([P, P], F32)
        nc.vector.memset(shift[:], 0.0)
        nc.vector.tensor_copy(out=shift[:, 0 : P - 1], in_=ident[:, 1:P])
        shiftb = const.tile([P, P], BF16)
        nc.vector.tensor_copy(out=shiftb[:], in_=shift[:])
        most = const.tile([P, P], BF16)
        nc.vector.tensor_scalar(
            out=most[:],
            in0=ident[:, P - 1 : P].to_broadcast([P, P]),
            scalar1=-1.0,
            scalar2=1.0,
            op0=ALU.mult,
            op1=ALU.add,
        )

        nc.vector.tensor_scalar(out=bbig[:], in0=bcol[:], scalar1=BIG, scalar2=None, op0=ALU.mult)

        ctx.enter_context(tc.manual_schedule())

        wraw = wprep.tile([P, 8 * D], BF16, offset=0)
        wg = {}
        for i in range(4):
            part = wprep.tile([P, 2 * D], BF16, align_bytes=64, offset=(16 + 4 * i) * D, name="wg%d" % i)
            wg[i // 2, i % 2] = part
        wrf = wraw[:].bitcast(F32)
        wc = const.tile([P, 2 * D], U32, align_bytes=64)
        ws = const.tile([P, 2 * D], U8, align_bytes=64)
        xraw = {}

        def load_w(u, v):
            nc.sync.dma_start(
                out=wraw[:, u * D : v * D].rearrange("p (j k) -> p j k", j=v - u), in_=wv[:, u:v, :]
            )

        def load_x(c, u, v):
            if u == 0:
                xr = xpool.tile([P, 4 * D], BF16, tag="xr")
                xraw[c] = xr
            nc.sync.dma_start(
                out=xraw[c][:, u * D : v * D].rearrange("p (t k) -> p t k", t=v - u),
                in_=xv[:, 4 * c + u : 4 * c + v, :],
            )

        load_x(0, 0, 1)
        for u, v in ((0, 2), (2, 4), (4, 6), (6, 7), (7, 8)):
            load_w(u, v)
        load_x(0, 1, 2)
        load_x(0, 2, 4)
        for c in range(1, 4):
            load_x(c, 0, 4)

        def words(t):
            return xraw[t // 4][:].bitcast(F32)[:, (t % 4) * HALF : (t % 4 + 1) * HALF]

        sacc = const.tile([P, 2 * NT], F32)
        nsq = const.tile([P, NT], F32)
        stot = const.tile([P, NT], F32)
        rsq = const.tile([P, NT], F32)
        rn = const.tile([P, NT], F32)
        rr = const.tile([P, NT + 1], F32)
        ar = const.tile([P, NT + 1], F32)
        dd = const.tile([P, TPP], F32)
        ad = const.tile([P, TPP], F32)
        ef = const.tile([P, 2, TPP], F32)
        r1 = const.tile([P, 2, TPP], F32)
        cf = const.tile([P, 2, TPP, NPIECE], BF16)
        junk = const.tile([P, D], BF16)
        sall = const.tile([P, NT, D], BF16)
        ylow = const.tile([P, YLOW, D], BF16)
        yhigh = wprep.tile([P, TPP - YLOW, D], BF16, offset=0)

        def ysl(u, v):
            return ylow[:, u:v, :] if v <= YLOW else yhigh[:, u - YLOW : v - YLOW, :]

        def keep_warm(n, u=0):
            for _ in range(n):
                nc.tensor.matmul(
                    out=acc[:, u:HALF], lhsT=unit[:, 0:P], rhs=unit[:, u:HALF], start=True, stop=True
                )

        def prep_w(u, v):
            h = u // 4
            for g in range(2):
                tp = psm.tile([P, HALF], F32, tag="mm")
                for j in range(u, v):
                    for c in range(2):
                        lo = ((j - u) * 2 + c) * P
                        at = j * HALF + (2 * g + c) * P
                        nc.tensor.transpose(tp[:, lo : lo + P], wrf[:, at : at + P], ident[:])
                dst = wg[h, g][:].bitcast(F32)[:, (u - 4 * h) * 2 * P : (v - 4 * h) * 2 * P]
                src = tp[:, 0 : (v - u) * 2 * P].rearrange("p (j w r) -> p j r w", j=v - u, w=2)
                copy = nc.scalar.copy if g == 0 else nc.vector.tensor_copy
                copy(out=dst.rearrange("p (j r w) -> p j r w", j=v - u, w=2), in_=src)

        def quant_w(h):
            for g in range(2):
                lo = g * D + h * HALF
                nc.vector.quantize_mx(
                    out=wc[:, lo : lo + HALF].bitcast(FP8X4), scales=ws[:, lo : lo + HALF], in_=wg[h, g][:]
                )

        tps = {}
        grp = {}
        cods = {}
        mmt = {}
        outs = {}

        def stage_t(k, a):
            if k < NG:
                tp = pst.tile([P, 4, P], F32, tag="tp")
                src = words(2 * k + a)
                for c in range(4):
                    nc.tensor.transpose(tp[:, c, :], src[:, c * P : (c + 1) * P], ident[:])
                tps[k, a] = tp

        def stage_ev(k, a, copy=nc.scalar.copy):
            if k < NG:
                if a == 0:
                    gt = gpool.tile([P, 2 * D], BF16, tag="grp", align_bytes=64)
                    grp[k] = gt
                gf = grp[k][:].bitcast(F32).rearrange("p (a g r u) -> p a g r u", a=2, g=2, u=2)
                copy(out=gf[:, a], in_=tps[k, a][:].rearrange("p (g u) r -> p g r u", u=2))

        def stage_q(k, part=(0, 2)):
            if k < NG:
                if part[0] == 0:
                    cod = cpool.tile([P, 512], U32, tag="cod", align_bytes=64)
                    scl = cpool.tile([P, 512], U8, tag="scl", align_bytes=64)
                    cods[k] = (cod, scl)
                cod, scl = cods[k]
                u, v = part
                nc.vector.quantize_mx(
                    out=cod[:, u * 256 : v * 256].bitcast(FP8X4),
                    scales=scl[:, u * 256 : v * 256],
                    in_=grp[k][:, u * D : v * D],
                )

        def stage_m(k, a, h):
            if k < NG:
                cod, scl = cods[k]
                mm = psm.tile([P, HALF], F32, tag="mm")
                for g in range(2):
                    off = (a * 2 + g) * P
                    lo = g * D + h * HALF
                    nc.tensor.matmul_mx(
                        out=mm[:],
                        lhsT=cod[:, off : off + P].bitcast(FP8X4),
                        lhsT_scale=scl[:, off : off + P],
                        rhs=wc[:, lo : lo + HALF].bitcast(FP8X4),
                        rhs_scale=ws[:, lo : lo + HALF],
                        start=(g == 0),
                        stop=(g == 1),
                    )
                mmt[k, a, h] = mm

        def stage_add(k, a, h):
            t = 2 * k + a
            if t not in outs:
                o = opool.tile([P, D], F32, tag="o")
                outs[t] = o
            nc.vector.scalar_tensor_tensor(
                out=outs[t][:, h * HALF : (h + 1) * HALF],
                in0=mmt[k, a, h][:],
                scalar=BIG,
                in1=bias[:, h * HALF : (h + 1) * HALF],
                op0=ALU.mult,
                op1=ALU.add,
                accum_out=sacc[:, h * NT + t : h * NT + t + 1],
            )

        def stage_square(t):
            nc.scalar.activation(out=junk[:], in_=outs[t][:], func=ACT.Square, scale=1.0 / BIG, accum_out=nsq[:, t : t + 1])

        def sign_vector(t, n):
            nc.vector.tensor_scalar(
                out=sall[:, t, 0:n], in0=outs[t][:, 0:n], scalar1=1.0, scalar2=-1.0, op0=ALU.min, op1=ALU.max
            )

        def sign_scalar(t, u=0):
            nc.scalar.activation(out=sall[:, t, u:D], in_=outs[t][:, u:D], func=ACT.Sign)

        shifted = const.tile([P, D], BF16)

        def shift_signs():
            for h in range(2):
                cols = slice(h * HALF, (h + 1) * HALF)
                mm = psm.tile([P, HALF], F32, tag="mm")
                nc.tensor.matmul(out=mm[:], lhsT=shiftb[:], rhs=sall[:, 0, cols], start=True, stop=True)
                nc.scalar.copy(out=shifted[:, cols], in_=mm[:])

        def products(u, v):
            nc.vector.tensor_tensor(
                out=ysl(u, v), in0=sall[:, u:v, :], in1=sall[:, u + 1 : v + 1, :], op=ALU.mult
            )

        def magnitude(cols):
            nc.vector.scalar_tensor_tensor(
                out=ar[:, cols], in0=rr[:, cols], scalar=-1.0, in1=rr[:, cols], op0=ALU.mult, op1=ALU.max
            )

        def fresh(b):
            lo, hi = BATCHES[b]
            return slice(lo if b == 0 else lo + 1, min(hi + 1, NT))

        def chain(b):
            lo, hi = BATCHES[b]
            new = fresh(b)
            cur = slice(lo, hi)
            nxt = slice(lo + 1, hi + 1)
            v = nc.vector

            def total():
                v.tensor_tensor(
                    out=stot[:, new], in0=sacc[:, new], in1=sacc[:, NT + new.start : NT + new.stop], op=ALU.add
                )

            def factor():
                v.scalar_tensor_tensor(
                    out=rr[:, new], in0=rn[:, new], scalar=1e8, in1=stot[:, new], op0=ALU.min, op1=ALU.mult
                )

            def difference():
                v.tensor_tensor(out=dd[:, cur], in0=rr[:, nxt], in1=rr[:, cur], op=ALU.subtract)
                magnitude(new)

            def larger():
                v.scalar_tensor_tensor(
                    out=ad[:, cur], in0=dd[:, cur], scalar=-1.0, in1=dd[:, cur], op0=ALU.mult, op1=ALU.max
                )
                v.tensor_tensor(out=ef[:, 1, cur], in0=ar[:, nxt], in1=ar[:, cur], op=ALU.max)

            def weight():
                v.tensor_tensor(out=ef[:, 0, cur], in0=ad[:, cur], in1=ef[:, 1, cur], op=ALU.subtract)

            def first_piece():
                v.tensor_copy(out=cf[:, :, cur, 0], in_=ef[:, :, cur])

            def second_piece():
                v.tensor_tensor(out=r1[:, :, cur], in0=ef[:, :, cur], in1=cf[:, :, cur, 0], op=ALU.subtract)
                v.tensor_tensor(out=cf[:, :, cur, 1], in0=ef[:, :, cur], in1=cf[:, :, cur, 0], op=ALU.subtract)

            def third_piece():
                v.tensor_tensor(out=cf[:, :, cur, 2], in0=r1[:, :, cur], in1=cf[:, :, cur, 1], op=ALU.subtract)

            return [total, factor, difference, larger, weight, first_piece, second_piece, third_piece]

        def inverse_norm(b):
            new = fresh(b)
            nc.vector.reciprocal(out=rsq[:, new], in_=nsq[:, new])
            nc.scalar.activation(out=rn[:, new], in_=rsq[:, new], func=ACT.Sqrt)

        def wrap_factor():
            nc.tensor.matmul(out=acc[:, RCOL : RCOL + 1], lhsT=shift[:], rhs=rr[:, 0:1], start=True, stop=True)

        def wrap_magnitude():
            wrap = slice(NT, NT + 1)
            nc.vector.tensor_copy(out=rr[:, wrap], in_=acc[:, RCOL : RCOL + 1])
            magnitude(wrap)

        def weigh(b):
            lo, hi = BATCHES[b]

            def block(j):
                col = (b * 8 + j) * NPIECE
                for pair in range(lo, hi):
                    nc.tensor.matmul(
                        out=acc[:, col : col + NPIECE],
                        lhsT=ysl(pair, pair + 1)[:, 0, j * P : (j + 1) * P],
                        rhs=cf[:, 0, pair, :],
                        start=(pair == lo),
                        stop=(pair == hi - 1),
                    )

            def constant(u, v, stationary):
                nc.tensor.matmul(
                    out=acc[:, YCOLS + u * NPIECE : YCOLS + v * NPIECE],
                    lhsT=stationary[:],
                    rhs=cf[:, 1, u:v, :].rearrange("p t c -> p (t c)"),
                    start=True,
                    stop=True,
                )

            steps = [lambda j=j: block(j) for j in range(8)]
            if b == 1:
                for i in (1, 2, 4, 6):
                    steps[i : i + 1] = [steps[i], lambda: keep_warm(2, RCOL + 2)]
            steps.append(lambda: constant(lo, min(hi, TPP - 1), ones))
            if hi == TPP:
                steps.append(lambda: constant(TPP - 1, TPP, most))
            return steps

        vq = []
        pq = []

        def trickle(queue, n):
            for _ in range(min(n, len(queue))):
                queue.pop(0)()

        keep_warm(WARMUP)
        stage_t(0, 0)
        stage_ev(0, 0)
        stage_q(0, (0, 1))
        bb = pst.tile([P, 8, P], BF16, tag="tp")
        for c in range(8):
            nc.tensor.transpose(bb[:, c, :], bbig[:, c : c + 1].to_broadcast([P, P]), identb[:])
        nc.scalar.copy(out=bias[:].rearrange("p (r c) -> p r c", c=8), in_=bb[:].rearrange("p c r -> p r c"))
        keep_warm(1)
        prep_w(0, 2)
        keep_warm(2)
        prep_w(2, 4)
        keep_warm(2)
        quant_w(0)
        prep_w(4, 6)
        keep_warm(2)
        prep_w(6, 8)
        stage_t(0, 1)
        stage_ev(0, 1)
        stage_m(0, 0, 0)
        quant_w(1)
        stage_t(1, 0)
        stage_ev(1, 0)
        stage_t(1, 1)
        stage_ev(1, 1)
        stage_m(0, 0, 1)
        stage_add(0, 0, 0)
        stage_q(0, (1, 2))
        stage_add(0, 0, 1)
        stage_m(0, 1, 0)
        stage_m(0, 1, 1)
        stage_q(1)
        stage_square(0)
        stage_t(2, 0)
        stage_ev(2, 0)
        stage_t(2, 1)
        stage_add(0, 1, 0)
        stage_add(0, 1, 1)
        stage_ev(2, 1)
        stage_m(1, 0, 0)
        stage_t(3, 0)
        stage_ev(3, 0)
        stage_t(3, 1)
        stage_m(1, 0, 1)
        sign_vector(0, VCOLS)
        stage_q(2)
        sign_scalar(0, VCOLS)
        stage_square(1)
        stage_m(1, 1, 0)
        stage_t(4, 0)
        stage_ev(3, 1)
        stage_m(1, 1, 1)
        stage_t(4, 1)
        sign_scalar(1)
        stage_m(2, 0, 0)
        load_x(4, 0, 4)

        for k in range(1, NG):
            if k % 2 == 0 and k // 2 + 4 < 8:
                load_x(k // 2 + 4, 0, 4)
            share = VCOLS if k < NG - 3 else 0 if k < NG - 1 else D
            stage_add(k, 0, 0)
            trickle(vq, 1)
            stage_ev(k + 3, 0)
            stage_m(k + 1, 0, 1)
            stage_add(k, 0, 1)
            for b, (lo, hi) in enumerate(BATCHES[:-1]):
                if k == hi // 2 + 1:
                    inverse_norm(b)
                    vq.extend(chain(b))
                if k == hi // 2 + (4 if b == 0 else 2):
                    pq.extend(weigh(b))
                    if b == 0:
                        pq.append(wrap_factor)
            stage_m(k + 1, 1, 0)
            stage_t(k + 4, 0)
            stage_square(2 * k)
            stage_q(k + 2)
            trickle(vq, 1)
            if share > 0:
                sign_vector(2 * k, share)
                trickle(vq, 1)
            stage_add(k, 1, 0)
            trickle(vq, 1)
            stage_ev(k + 3, 1)
            if share < D:
                sign_scalar(2 * k, share)
            stage_m(k + 1, 1, 1)
            if k < NG - 1:
                trickle(pq, 3)
            stage_t(k + 4, 1)
            stage_add(k, 1, 1)
            trickle(vq, 1)
            stage_m(k + 2, 0, 0)
            if k == NG - 2:
                wrap_magnitude()
                shift_signs()
            products(max(2 * k - 3, 0), 2 * k - 1 if k < NG - 1 else 2 * k)
            if k < NG - 1:
                stage_square(2 * k + 1)
                sign_scalar(2 * k + 1)
            trickle(pq, 3)

        stage_square(NT - 1)
        inverse_norm(NB - 1)
        last = chain(NB - 1)
        sign_scalar(NT - 1)
        trickle(vq, len(vq))
        trickle(pq, len(pq))
        keep_warm(COOL, RCOL + 2)

        def late_product(pair, h):
            cols = slice(h * HALF, (h + 1) * HALF)
            following = shifted[:, cols] if pair == NT - 1 else sall[:, pair + 1, cols]
            nc.vector.tensor_tensor(out=ysl(pair, pair + 1)[:, 0, cols], in0=following, in1=sall[:, pair, cols], op=ALU.mult)

        fillers = [(pair, h) for pair in (NT - 2, NT - 1) for h in range(2)]
        for i in range(len(last)):
            trickle(last, 1)
            if i >= 3 and fillers:
                late_product(*fillers.pop(0))
        base = const.tile([P, 1], F32)
        cs = const.tile([P, 1], F32)
        ysum = const.tile([P, 8], F32)
        res = const.tile([P, D], F32)
        accy = acc[:, 0:YCOLS].rearrange("p (b j c) -> p j b c", b=NB, j=8, c=NPIECE)
        scale = 1.0 / (32.0 * BIG)
        final = weigh(NB - 1)
        for step in final[0:4] + final[8:]:
            step()
        for h in range(2):
            js = slice(4 * h, 4 * h + 4)
            nc.vector.tensor_reduce(out=ysum[:, js], in_=accy[:, js], axis=AX.XY, op=ALU.add)
            if h == 0:
                nc.vector.tensor_reduce(
                    out=cs[:], in_=acc[:, YCOLS : YCOLS + TPP * NPIECE], axis=AX.X, op=ALU.add
                )
                nc.vector.tensor_scalar(out=base[:], in0=cs[:], scalar1=scale, scalar2=None, op0=ALU.mult)
            for q in range(2):
                bc = psm.tile([P, HALF], F32, tag="mm")
                for i in range(2):
                    j = 4 * h + 2 * q + i
                    nc.tensor.transpose(
                        bc[:, i * P : (i + 1) * P], ysum[:, j : j + 1].to_broadcast([P, P]), ident[:]
                    )
                cols = slice((4 * h + 2 * q) * P, (4 * h + 2 * q + 2) * P)
                if q == 1:
                    nc.scalar.activation(
                        out=res[:, cols], in_=bc[:, 0 : 2 * P], func=ACT.Identity, scale=scale, bias=base[:, 0:1]
                    )
                else:
                    nc.vector.tensor_scalar(
                        out=res[:, cols],
                        in0=bc[:, 0 : 2 * P],
                        scalar1=scale,
                        scalar2=base[:, 0:1],
                        op0=ALU.mult,
                        op1=ALU.add,
                    )
            for i in range(2):
                eng = nc.sync if i == 0 else nc.scalar
                cols = slice(h * HALF, (h + 1) * HALF)
                eng.dma_start(
                    out=out[4 * i * P : 4 * (i + 1) * P, cols].rearrange("(e p) d -> p e d", p=P),
                    in_=res[:, cols].unsqueeze(1).to_broadcast([P, 4, HALF]),
                )
            if h == 0:
                for step in final[4:8]:
                    step()
